import numpy as np
import ml_dtypes


def mxq(x, axis, fmt="e4m3"):
    dtype, down = {"e4m3": (ml_dtypes.float8_e4m3fn, 7), "e5m2": (ml_dtypes.float8_e5m2, 14)}[fmt]
    v = np.moveaxis(np.asarray(x, np.float32).astype(ml_dtypes.bfloat16).astype(np.float64), axis, -1)
    blocks = v.reshape(v.shape[:-1] + (-1, 32))
    amax = np.abs(blocks).max(-1, keepdims=True)
    byte = np.maximum(np.where(amax > 0, np.frexp(amax)[1] - 1 + 127, 0) - down, 1)
    scale = np.exp2(byte - 127.0)
    codes = (blocks / scale).astype(np.float32).astype(dtype).astype(np.float64)
    return np.moveaxis((codes * scale).reshape(v.shape), -1, axis)


WIDE = False


def mx_kscale(k):
    if not WIDE:
        return np.ones(k)
    levels = np.array([20, -20, 10, -10, 0])
    a = np.random.permutation(np.resize(levels, k // 512 * 4)).reshape(k // 512, 4)
    idx = np.arange(k)
    return np.exp2(a[idx // 512, idx % 128 // 32])


BF16 = ml_dtypes.bfloat16


def bf(x):
    return np.asarray(x, np.float32).astype(BF16)


def f64(x):
    return np.asarray(x).astype(np.float64)


B, I, O, G = 8192, 128, 512, 8


def setup_inputs():
    u = mx_kscale(O)
    x = np.random.random((B, I))
    w = np.random.standard_normal((I * G, O)) * 2.0 / np.sqrt(I * G) / u[None, :]
    bw = np.random.standard_normal((O, I)) / np.sqrt(I) / u[:, None]
    grid = np.linspace(0.0, 1.0, G)
    g = np.random.standard_normal((B, O)) * np.exp2(np.random.randint(-12, 1, (B, 1))) * 4.0 * u[None, :]
    return {"x": bf(x), "spline_weight": bf(w), "base_weight": bf(bw), "grid": bf(grid), "grad_out": bf(g)}


def reference(x, spline_weight, base_weight, grid, grad_out):
    x = f64(x)
    gq = mxq(f64(grad_out), 1, "e5m2")
    g_base = gq @ mxq(f64(base_weight), 0, "e4m3")
    g_basis = gq @ mxq(f64(spline_weight), 1, "e4m3").T
    g_basis = g_basis.reshape(x.shape[0], x.shape[1], -1)
    d = x[:, :, None] - f64(grid)[None, None, :]
    dbasis = -40.0 * d * np.exp(-20.0 * d ** 2)
    return g_base + (g_basis * dbasis).sum(axis=2)

@@ -1,0 +1,312 @@
+from contextlib import ExitStack
+
+import concourse.mybir as mybir
+from concourse.masks import make_identity
+
+F32 = mybir.dt.float32
+BF16 = mybir.dt.bfloat16
+U32 = mybir.dt.uint32
+U8 = mybir.dt.uint8
+E4X4 = mybir.dt.float8_e4m3fn_x4
+E5X4 = mybir.dt.float8_e5m2_x4
+ACT = mybir.ActivationFunctionType
+ALU = mybir.AluOpType
+
+P = 128
+B, I, O, G = 8192, 128, 512, 8
+NT = B // P
+SPAN_T = 8
+SPAN = SPAN_T * P
+HALF = SPAN // 2
+NSPAN = NT // SPAN_T
+FLOPS = 2 * B * O * (I + I * G)
+
+PIN = True
+LAG = 3
+S_AHEAD = 3
+E_BUFS = 5
+R_BUFS = 6
+Q_BUFS = 3
+ACC_BUFS = 3
+TP_BUFS = 2
+G_ORDER = [0,1,2,3,4,5,6,7,8]
+NJ = G + 1
+
+
+def mult_on_vector(s, g):
+    return g == 7
+
+
+def tile_rbfkanlayer_t_kernel(tc, x, spline_weight, base_weight, grid, grad_out, out):
+    nc = tc.nc
+    xv = x.rearrange("(p t) i -> p t i", t=NT)
+    gv = grad_out.rearrange("(p t) o -> p t o", t=NT)
+    ov = out.rearrange("(p t) i -> p t i", t=NT)
+    wv = spline_weight.rearrange("(i g) o -> i g o", g=G)
+
+    with ExitStack() as ctx:
+        const = ctx.enter_context(tc.tile_pool(name="const", bufs=1))
+        gpool = ctx.enter_context(tc.tile_pool(name="gpool", bufs=NSPAN))
+        xtpool = ctx.enter_context(tc.tile_pool(name="xtpool", bufs=NSPAN))
+        gqpool = ctx.enter_context(tc.tile_pool(name="gqpool", bufs=2))
+        gcpool = ctx.enter_context(tc.tile_pool(name="gcpool", bufs=2))
+        epool = ctx.enter_context(tc.tile_pool(name="epool", bufs=E_BUFS))
+        rpool = ctx.enter_context(tc.tile_pool(name="rpool", bufs=R_BUFS))
+        opool = ctx.enter_context(tc.tile_pool(name="opool", bufs=2))
+        tp = ctx.enter_context(tc.psum_pool(name="tp", bufs=TP_BUFS))
+        qp = ctx.enter_context(tc.psum_pool(name="qp", bufs=Q_BUFS))
+        accp = ctx.enter_context(tc.psum_pool(name="accp", bufs=ACC_BUFS))
+        if PIN:
+            ctx.enter_context(tc.manual_schedule())
+
+        grid_bf = const.tile([P, G], BF16, name="grid_bf")
+        nc.sync.dma_start(out=grid_bf[:], in_=grid.partition_broadcast(P))
+        x_first = const.tile([P, SPAN_T, I], BF16, name="x_first")
+        nc.sync.dma_start(out=x_first[:], in_=xv[:, 0:SPAN_T, :])
+        w_a = const.tile([P, 2, O], BF16, name="w_a")
+        nc.sync.dma_start(out=w_a[:], in_=wv[:, 0:2, :])
+        g_sb = []
+        g_t = gpool.tile([P, SPAN_T, O], BF16, name="g_sb", tag="g_sb")
+        g_sb.append(g_t)
+        nc.sync.dma_start(out=g_t[:, 0:4, :], in_=gv[:, 0:4, :])
+        nc.sync.dma_start(out=g_t[:, 4:8, :], in_=gv[:, 4:8, :])
+        w_b = const.tile([P, G - 2, O], BF16, name="w_b")
+        nc.sync.dma_start(out=w_b[:], in_=wv[:, 2:G, :])
+        wb_raw = const.tile([P, 4, I], BF16, name="wb_raw")
+        for u in range(2):
+            nc.sync.dma_start(
+                out=wb_raw[:, 2 * u : 2 * u + 2, :],
+                in_=base_weight[256 * u : 256 * u + 256, :].rearrange("(p e) c -> p e c", e=2),
+            )
+        x_rest = const.tile([P, NT - SPAN_T, I], BF16, name="x_rest")
+        nc.sync.dma_start(out=x_rest[:], in_=xv[:, SPAN_T:NT, :])
+        for s in range(1, NSPAN):
+            g_t = gpool.tile([P, SPAN_T, O], BF16, name="g_sb", tag="g_sb")
+            nc.sync.dma_start(out=g_t[:], in_=gv[:, s * SPAN_T : (s + 1) * SPAN_T, :])
+            g_sb.append(g_t)
+
+        def w_rows(g):
+            return w_a[:, g, :] if g < 2 else w_b[:, g - 2, :]
+
+        def x_rows(t):
+            return x_first[:, t, :] if t < SPAN_T else x_rest[:, t - SPAN_T, :]
+
+        ident_b = const.tile([P, P], BF16, name="ident_b")
+        make_identity(nc, ident_b[:])
+        ident_f = const.tile([P, P], F32, name="ident_f")
+        make_identity(nc, ident_f[:])
+        c_pos = const.tile([P, G], F32, name="c_pos")
+        nc.vector.tensor_copy(out=c_pos[:], in_=grid_bf[:])
+        c_neg = const.tile([P, G], F32, name="c_neg")
+        nc.vector.tensor_scalar_mul(out=c_neg[:], in0=grid_bf[:], scalar1=-1.0)
+
+        xT = {}
+        g_codes = {}
+
+        def words_pe(src0, src1):
+            ps = tp.tile([P, 2, 2 * P], F32, name="ps_w", tag="tp")
+            for j, src in enumerate((src0, src1)):
+                for u in range(2):
+                    nc.tensor.transpose(
+                        out=ps[:, u, j * P : (j + 1) * P],
+                        in_=src.bitcast(F32)[:, u * P : (u + 1) * P],
+                        identity=ident_f[:],
+                    )
+            return ps
+
+        def words_copy(ps, dst):
+            nc.vector.tensor_copy(out=dst, in_=ps[:].rearrange("p u n -> p n u"))
+
+        def prep_tasks(s):
+            tasks = []
+
+            def x_pe():
+                ps = tp.tile([P, SPAN], BF16, name="ps_x", tag="tp")
+                for tt in range(SPAN_T):
+                    nc.tensor.transpose(
+                        out=ps[:, tt * P : (tt + 1) * P], in_=x_rows(s * SPAN_T + tt), identity=ident_b[:]
+                    )
+                return ps
+
+            def x_copy(ps):
+                xt = xtpool.tile([P, SPAN], BF16, name="xT", tag="xT")
+                nc.vector.tensor_copy(out=xt[:], in_=ps[:])
+                xT[s] = xt
+
+            tasks.append((x_pe, x_copy))
+            gq = gqpool.tile([P, 4 * SPAN], BF16, name="gq", tag="gq", align_bytes=64)
+            gq_f = gq[:].bitcast(F32).rearrange("p (n u) -> p n u", u=2)
+            gc = gcpool.tile([P, SPAN], U32, name="gc", tag="gc", align_bytes=64)
+            gs = gcpool.tile([P, SPAN], U8, name="gs", tag="gs", align_bytes=64)
+            g_codes[s] = (gc, gs)
+            for b in range(4):
+                tasks.append(
+                    (
+                        lambda b=b: words_pe(g_sb[s][:, 2 * b, :], g_sb[s][:, 2 * b + 1, :]),
+                        lambda ps, b=b: words_copy(ps, gq_f[:, 2 * P * b : 2 * P * (b + 1), :]),
+                    )
+                )
+                if b % 2 == 1:
+                    h = b // 2
+                    tasks.append(
+                        (
+                            lambda: None,
+                            lambda ps, h=h: nc.vector.quantize_mx(
+                                out=gc[:, h * HALF : (h + 1) * HALF].bitcast(E5X4),
+                                scales=gs[:, h * HALF : (h + 1) * HALF],
+                                in_=gq[:, 4 * h * HALF : 4 * (h + 1) * HALF],
+                            ),
+                        )
+                    )
+            return tasks
+
+        wq = const.tile([P, 4 * NJ * I], BF16, name="wq", align_bytes=64)
+        wc = const.tile([P, NJ * I], U32, name="wc", align_bytes=64)
+        ws = const.tile([P, NJ * I], U8, name="ws", align_bytes=64)
+        wq_f = wq[:, 0 : 4 * G * I].bitcast(F32).rearrange("p (n u) -> p n u", u=2)
+
+        def w_quant(c0, c1):
+            nc.vector.quantize_mx(
+                out=wc[:, c0:c1].bitcast(E4X4), scales=ws[:, c0:c1], in_=wq[:, 4 * c0 : 4 * c1]
+            )
+
+        def w_pairs(pairs):
+            for b in pairs:
+                ps = words_pe(w_rows(2 * b), w_rows(2 * b + 1))
+                words_copy(ps, wq_f[:, 2 * P * b : 2 * P * (b + 1), :])
+            w_quant(2 * I * pairs[0], 2 * I * (pairs[-1] + 1))
+
+        def w_base():
+            nc.vector.tensor_copy(
+                out=wq[:, 4 * G * I : 4 * NJ * I].rearrange("p (c t) -> p c t", t=4),
+                in_=wb_raw[:].rearrange("p t c -> p c t"),
+            )
+            w_quant(G * I, NJ * I)
+
+        first = prep_tasks(0)
+        first[0][1](first[0][0]())
+        w_pairs([0])
+        for pe_part, v_part in first[1:]:
+            v_part(pe_part())
+        head_rest = [lambda: w_pairs([1]), lambda: w_pairs([2, 3]), w_base]
+
+        units = [(s, g) for s in range(NSPAN) for g in G_ORDER]
+        NU = len(units)
+        e_of = {}
+        q_of = {}
+        r_of = {}
+        acc_of = {}
+
+        def emit_scalar(k):
+            if k >= NU:
+                return
+            s, g = units[k]
+            if g == G:
+                return
+            e = epool.tile([P, SPAN], F32, name="e", tag="e")
+            e_of[k] = e
+            nc.scalar.activation(out=e[:], in_=xT[s][:], func=ACT.Square, bias=c_neg[:, g : g + 1], scale=1.0)
+            nc.scalar.activation(out=e[:], in_=e[:], func=ACT.Exp, scale=-20.0)
+
+        def emit_mx(k):
+            s, g = units[k]
+            gc, gs = g_codes[s]
+            qs = []
+            for h in range(2):
+                q = qp.tile([P, HALF], F32, name="q", tag="q")
+                nc.tensor.matmul_mx(
+                    out=q[:],
+                    lhsT=wc[:, g * I : (g + 1) * I].bitcast(E4X4),
+                    lhsT_scale=ws[:, g * I : (g + 1) * I],
+                    rhs=gc[:, h * HALF : (h + 1) * HALF].bitcast(E5X4),
+                    rhs_scale=gs[:, h * HALF : (h + 1) * HALF],
+                    start=True,
+                    stop=True,
+                )
+                qs.append(q)
+            q_of[k] = qs
+
+        def emit_evac(k):
+            s, g = units[k]
+            r = rpool.tile([P, SPAN], F32, name="r", tag="r")
+            r_of[k] = r
+            for h in range(2):
+                if g < G:
+                    nc.vector.scalar_tensor_tensor(
+                        out=r[:, h * HALF : (h + 1) * HALF],
+                        in0=xT[s][:, h * HALF : (h + 1) * HALF],
+                        scalar=c_pos[:, g : g + 1],
+                        in1=q_of[k][h][:],
+                        op0=ALU.subtract,
+                        op1=ALU.mult,
+                    )
+                else:
+                    nc.vector.tensor_scalar_mul(
+                        out=r[:, h * HALF : (h + 1) * HALF], in0=q_of[k][h][:], scalar1=-1.0 / 40.0
+                    )
+
+        def emit_mult(k):
+            s, g = units[k]
+            if g == G:
+                return
+            eng = nc.vector if mult_on_vector(s, g) else nc.gpsimd
+            eng.tensor_tensor(out=r_of[k][:], in0=r_of[k][:], in1=e_of[k][:], op=ALU.mult)
+
+        def emit_acc(k):
+            s, g = units[k]
+            j = k % NJ
+            if j == 0:
+                acc_of[s] = [accp.tile([P, HALF], F32, name="acc%d" % h, tag="acc") for h in range(2)]
+            for tt in range(SPAN_T):
+                nc.tensor.matmul(
+                    out=acc_of[s][tt // 4][:, (tt % 4) * P : (tt % 4 + 1) * P],
+                    lhsT=r_of[k][:, tt * P : (tt + 1) * P],
+                    rhs=ident_f[:],
+                    is_transpose=True,
+                    start=(j == 0 and tt % 4 == 0),
+                    stop=(j == NJ - 1 and tt % 4 == 3),
+                )
+
+        def emit_out(s):
+            o_sb = opool.tile([P, SPAN_T, I], F32, name="o_sb", tag="o_sb")
+            for h in range(2):
+                nc.vector.tensor_scalar_mul(
+                    out=o_sb[:, 4 * h : 4 * h + 4, :].rearrange("p t i -> p (t i)"),
+                    in0=acc_of[s][h][:],
+                    scalar1=-40.0,
+                )
+            nc.sync.dma_start(out=ov[:, s * SPAN_T : (s + 1) * SPAN_T, :], in_=o_sb[:])
+
+        for k in range(S_AHEAD):
+            emit_scalar(k)
+        tasks = []
+        task_i = 0
+        head_i = 0
+        pending = []
+        for k in range(NU + LAG):
+            s, j = k // NJ, k % NJ
+            emit_scalar(k + S_AHEAD)
+            if k < NU:
+                if j == 0 and s + 1 < NSPAN:
+                    tasks = prep_tasks(s + 1)
+                    task_i = 0
+                emit_mx(k)
+            if 0 <= k - LAG < NU:
+                emit_acc(k - LAG)
+            fresh = []
+            if k < NU and j >= 1 and task_i < len(tasks):
+                pe_part, v_part = tasks[task_i]
+                task_i += 1
+                fresh.append((v_part, pe_part()))
+            if k < NU:
+                emit_evac(k)
+            if head_i < len(head_rest):
+                head_rest[head_i]()
+                head_i += 1
+            for v_part, ps in pending:
+                v_part(ps)
+            pending = fresh
+            if k < NU:
+                emit_mult(k)
+            if 0 <= k - LAG < NU and (k - LAG) % NJ == NJ - 1:
+                emit_out((k - LAG) // NJ)

@@ -31,6 +31,7 @@ ACC_BUFS = 3
 TP_BUFS = 2
 G_ORDER = [0,1,2,3,4,5,6,7,8]
 NJ = G + 1
+DUP = 1
 
 
 def mult_on_vector(s, g):
@@ -214,7 +215,8 @@ def tile_rbfkanlayer_t_kernel(tc, x, spline_weight, base_weight, grid, grad_out,
             qs = []
             for h in range(2):
                 q = qp.tile([P, HALF], F32, name="q", tag="q")
-                nc.tensor.matmul_mx(
+                for rep in range(1 + (DUP if h == 0 else 0)):
+                  nc.tensor.matmul_mx(
                     out=q[:],
                     lhsT=wc[:, g * I : (g + 1) * I].bitcast(E4X4),
                     lhsT_scale=ws[:, g * I : (g + 1) * I],

@@ -23,19 +23,16 @@ FLOPS = 2 * B * O * (I + I * G)
 
 PIN = True
 LAG = 3
-S_AHEAD = 3
-E_BUFS = 5
-R_BUFS = 6
+S_AHEAD = 4
+E_BUFS = 8
+R_BUFS = 8
 Q_BUFS = 3
 ACC_BUFS = 3
 TP_BUFS = 2
-G_ORDER = [0,1,2,3,4,5,6,7,8]
 NJ = G + 1
-DUP = 1
-
-
-def mult_on_vector(s, g):
-    return g == 7
+N_GPSIMD = 5
+OUT_ON_SCALAR = True
+XT_ON_SCALAR = False
 
 
 def tile_rbfkanlayer_t_kernel(tc, x, spline_weight, base_weight, grid, grad_out, out):
@@ -131,7 +128,10 @@ def tile_rbfkanlayer_t_kernel(tc, x, spline_weight, base_weight, grid, grad_out,
 
             def x_copy(ps):
                 xt = xtpool.tile([P, SPAN], BF16, name="xT", tag="xT")
-                nc.vector.tensor_copy(out=xt[:], in_=ps[:])
+                if XT_ON_SCALAR and s > 0:
+                    nc.scalar.copy(out=xt[:], in_=ps[:])
+                else:
+                    nc.vector.tensor_copy(out=xt[:], in_=ps[:])
                 xT[s] = xt
 
             tasks.append((x_pe, x_copy))
@@ -147,19 +147,16 @@ def tile_rbfkanlayer_t_kernel(tc, x, spline_weight, base_weight, grid, grad_out,
                         lambda ps, b=b: words_copy(ps, gq_f[:, 2 * P * b : 2 * P * (b + 1), :]),
                     )
                 )
-                if b % 2 == 1:
-                    h = b // 2
-                    tasks.append(
-                        (
-                            lambda: None,
-                            lambda ps, h=h: nc.vector.quantize_mx(
-                                out=gc[:, h * HALF : (h + 1) * HALF].bitcast(E5X4),
-                                scales=gs[:, h * HALF : (h + 1) * HALF],
-                                in_=gq[:, 4 * h * HALF : 4 * (h + 1) * HALF],
-                            ),
-                        )
+
+            def quantise():
+                for h in range(2):
+                    nc.vector.quantize_mx(
+                        out=gc[:, h * HALF : (h + 1) * HALF].bitcast(E5X4),
+                        scales=gs[:, h * HALF : (h + 1) * HALF],
+                        in_=gq[:, 4 * h * HALF : 4 * (h + 1) * HALF],
                     )
-            return tasks
+
+            return tasks, quantise
 
         wq = const.tile([P, 4 * NJ * I], BF16, name="wq", align_bytes=64)
         wc = const.tile([P, NJ * I], U32, name="wc", align_bytes=64)
@@ -184,15 +181,16 @@ def tile_rbfkanlayer_t_kernel(tc, x, spline_weight, base_weight, grid, grad_out,
             )
             w_quant(G * I, NJ * I)
 
-        first = prep_tasks(0)
+        first, first_quantise = prep_tasks(0)
         first[0][1](first[0][0]())
         w_pairs([0])
         for pe_part, v_part in first[1:]:
             v_part(pe_part())
+        first_quantise()
         head_rest = [lambda: w_pairs([1]), lambda: w_pairs([2, 3]), w_base]
 
-        units = [(s, g) for s in range(NSPAN) for g in G_ORDER]
-        NU = len(units)
+        NU = NSPAN * NJ
+        NB = 2 * NU
         e_of = {}
         q_of = {}
         r_of = {}
@@ -201,7 +199,7 @@ def tile_rbfkanlayer_t_kernel(tc, x, spline_weight, base_weight, grid, grad_out,
         def emit_scalar(k):
             if k >= NU:
                 return
-            s, g = units[k]
+            s, g = k // NJ, k % NJ
             if g == G:
                 return
             e = epool.tile([P, SPAN], F32, name="e", tag="e")
@@ -209,54 +207,47 @@ def tile_rbfkanlayer_t_kernel(tc, x, spline_weight, base_weight, grid, grad_out,
             nc.scalar.activation(out=e[:], in_=xT[s][:], func=ACT.Square, bias=c_neg[:, g : g + 1], scale=1.0)
             nc.scalar.activation(out=e[:], in_=e[:], func=ACT.Exp, scale=-20.0)
 
-        def emit_mx(k):
-            s, g = units[k]
-            gc, gs = g_codes[s]
-            qs = []
-            for h in range(2):
-                q = qp.tile([P, HALF], F32, name="q", tag="q")
-                for rep in range(1 + (DUP if h == 0 else 0)):
-                  nc.tensor.matmul_mx(
-                    out=q[:],
-                    lhsT=wc[:, g * I : (g + 1) * I].bitcast(E4X4),
-                    lhsT_scale=ws[:, g * I : (g + 1) * I],
-                    rhs=gc[:, h * HALF : (h + 1) * HALF].bitcast(E5X4),
-                    rhs_scale=gs[:, h * HALF : (h + 1) * HALF],
-                    start=True,
-                    stop=True,
-                )
-                qs.append(q)
-            q_of[k] = qs
-
-        def emit_evac(k):
-            s, g = units[k]
-            r = rpool.tile([P, SPAN], F32, name="r", tag="r")
-            r_of[k] = r
-            for h in range(2):
-                if g < G:
-                    nc.vector.scalar_tensor_tensor(
-                        out=r[:, h * HALF : (h + 1) * HALF],
-                        in0=xT[s][:, h * HALF : (h + 1) * HALF],
-                        scalar=c_pos[:, g : g + 1],
-                        in1=q_of[k][h][:],
-                        op0=ALU.subtract,
-                        op1=ALU.mult,
-                    )
-                else:
-                    nc.vector.tensor_scalar_mul(
-                        out=r[:, h * HALF : (h + 1) * HALF], in0=q_of[k][h][:], scalar1=-1.0 / 40.0
-                    )
-
-        def emit_mult(k):
-            s, g = units[k]
-            if g == G:
+        def emit_mx(n):
+            if n >= NB:
                 return
-            eng = nc.vector if mult_on_vector(s, g) else nc.gpsimd
+            k, h = n // 2, n % 2
+            s, g = k // NJ, k % NJ
+            gc, gs = g_codes[s]
+            q = qp.tile([P, HALF], F32, name="q", tag="q")
+            nc.tensor.matmul_mx(
+                out=q[:],
+                lhsT=wc[:, g * I : (g + 1) * I].bitcast(E4X4),
+                lhsT_scale=ws[:, g * I : (g + 1) * I],
+                rhs=gc[:, h * HALF : (h + 1) * HALF].bitcast(E5X4),
+                rhs_scale=gs[:, h * HALF : (h + 1) * HALF],
+                start=True,
+                stop=True,
+            )
+            q_of[n] = q
+
+        def emit_evac(n):
+            k, h = n // 2, n % 2
+            s, g = k // NJ, k % NJ
+            if h == 0:
+                r_of[k] = rpool.tile([P, SPAN], F32, name="r", tag="r")
+            r = r_of[k]
+            if g < G:
+                nc.vector.scalar_tensor_tensor(
+                    out=r[:, h * HALF : (h + 1) * HALF],
+                    in0=xT[s][:, h * HALF : (h + 1) * HALF],
+                    scalar=c_pos[:, g : g + 1],
+                    in1=q_of[n][:],
+                    op0=ALU.subtract,
+                    op1=ALU.mult,
+                )
+            else:
+                nc.vector.tensor_scalar_mul(out=r[:, h * HALF : (h + 1) * HALF], in0=q_of[n][:], scalar1=-1.0 / 40.0)
+
+        def emit_mult(eng, k):
             eng.tensor_tensor(out=r_of[k][:], in0=r_of[k][:], in1=e_of[k][:], op=ALU.mult)
 
         def emit_acc(k):
-            s, g = units[k]
-            j = k % NJ
+            s, j = k // NJ, k % NJ
             if j == 0:
                 acc_of[s] = [accp.tile([P, HALF], F32, name="acc%d" % h, tag="acc") for h in range(2)]
             for tt in range(SPAN_T):
@@ -272,43 +263,63 @@ def tile_rbfkanlayer_t_kernel(tc, x, spline_weight, base_weight, grid, grad_out,
         def emit_out(s):
             o_sb = opool.tile([P, SPAN_T, I], F32, name="o_sb", tag="o_sb")
             for h in range(2):
-                nc.vector.tensor_scalar_mul(
-                    out=o_sb[:, 4 * h : 4 * h + 4, :].rearrange("p t i -> p (t i)"),
-                    in0=acc_of[s][h][:],
-                    scalar1=-40.0,
-                )
+                dst = o_sb[:, 4 * h : 4 * h + 4, :].rearrange("p t i -> p (t i)")
+                if OUT_ON_SCALAR and s + 1 < NSPAN:
+                    nc.scalar.activation(out=dst, in_=acc_of[s][h][:], func=ACT.Copy, scale=-40.0)
+                else:
+                    nc.vector.tensor_scalar_mul(out=dst, in0=acc_of[s][h][:], scalar1=-40.0)
             nc.sync.dma_start(out=ov[:, s * SPAN_T : (s + 1) * SPAN_T, :], in_=o_sb[:])
 
         for k in range(S_AHEAD):
             emit_scalar(k)
+        emit_mx(0)
+        emit_mx(1)
         tasks = []
+        quantise_next = None
         task_i = 0
         head_i = 0
-        pending = []
-        for k in range(NU + LAG):
+        pending = None
+        out_pending = -1
+        for n in range(NB):
+            k, h = n // 2, n % 2
             s, j = k // NJ, k % NJ
-            emit_scalar(k + S_AHEAD)
-            if k < NU:
+            if h == 0:
+                emit_scalar(k + S_AHEAD)
                 if j == 0 and s + 1 < NSPAN:
-                    tasks = prep_tasks(s + 1)
+                    tasks, quantise_next = prep_tasks(s + 1)
                     task_i = 0
-                emit_mx(k)
-            if 0 <= k - LAG < NU:
-                emit_acc(k - LAG)
-            fresh = []
-            if k < NU and j >= 1 and task_i < len(tasks):
+            if j == G and h == 0:
+                if s + 1 < NSPAN:
+                    quantise_next()
+                for jj in range(N_GPSIMD, G):
+                    emit_mult(nc.vector, s * NJ + jj)
+                    emit_acc(s * NJ + jj)
+            emit_mx(n + 2)
+            if h == 1 and j < G:
+                if 0 <= j - LAG < N_GPSIMD:
+                    emit_acc(s * NJ + j - LAG)
+                if j == G - 1:
+                    for z in range(max(0, G - LAG), N_GPSIMD):
+                        emit_acc(s * NJ + z)
+            fresh = None
+            if h == 1 and j < G and task_i < len(tasks):
                 pe_part, v_part = tasks[task_i]
                 task_i += 1
-                fresh.append((v_part, pe_part()))
-            if k < NU:
-                emit_evac(k)
-            if head_i < len(head_rest):
-                head_rest[head_i]()
-                head_i += 1
-            for v_part, ps in pending:
-                v_part(ps)
-            pending = fresh
-            if k < NU:
-                emit_mult(k)
-            if 0 <= k - LAG < NU and (k - LAG) % NJ == NJ - 1:
-                emit_out((k - LAG) // NJ)
+                fresh = (v_part, pe_part())
+            emit_evac(n)
+            if h == 1:
+                if pending is not None:
+                    pending[0](pending[1])
+                pending = fresh
+                if head_i < len(head_rest):
+                    head_rest[head_i]()
+                    head_i += 1
+                if j < N_GPSIMD:
+                    emit_mult(nc.gpsimd, k)
+                if j == G:
+                    emit_acc(k)
+                    out_pending = s
+                if j == 0 and out_pending >= 0:
+                    emit_out(out_pending)
+                    out_pending = -1
+        emit_out(out_pending)

@@ -19,20 +19,17 @@ SPAN_T = 8
 SPAN = SPAN_T * P
 HALF = SPAN // 2
 NSPAN = NT // SPAN_T
+NJ = G + 1
+NU = NSPAN * NJ
+NB = 2 * NU
 FLOPS = 2 * B * O * (I + I * G)
-
-PIN = True
 LAG = 3
 S_AHEAD = 4
 E_BUFS = 8
 R_BUFS = 8
-Q_BUFS = 3
-ACC_BUFS = 3
-TP_BUFS = 2
-NJ = G + 1
-N_GPSIMD = 5
+N_GPSIMD = 4
 OUT_ON_SCALAR = True
-XT_ON_SCALAR = False
+XT_ON_SCALAR = True
 
 
 def tile_rbfkanlayer_t_kernel(tc, x, spline_weight, base_weight, grid, grad_out, out):
@@ -45,29 +42,36 @@ def tile_rbfkanlayer_t_kernel(tc, x, spline_weight, base_weight, grid, grad_out,
     with ExitStack() as ctx:
         const = ctx.enter_context(tc.tile_pool(name="const", bufs=1))
         gpool = ctx.enter_context(tc.tile_pool(name="gpool", bufs=NSPAN))
+        xpool = ctx.enter_context(tc.tile_pool(name="xpool", bufs=NSPAN))
         xtpool = ctx.enter_context(tc.tile_pool(name="xtpool", bufs=NSPAN))
         gqpool = ctx.enter_context(tc.tile_pool(name="gqpool", bufs=2))
         gcpool = ctx.enter_context(tc.tile_pool(name="gcpool", bufs=2))
         epool = ctx.enter_context(tc.tile_pool(name="epool", bufs=E_BUFS))
         rpool = ctx.enter_context(tc.tile_pool(name="rpool", bufs=R_BUFS))
         opool = ctx.enter_context(tc.tile_pool(name="opool", bufs=2))
-        tp = ctx.enter_context(tc.psum_pool(name="tp", bufs=TP_BUFS))
-        qp = ctx.enter_context(tc.psum_pool(name="qp", bufs=Q_BUFS))
-        accp = ctx.enter_context(tc.psum_pool(name="accp", bufs=ACC_BUFS))
-        if PIN:
-            ctx.enter_context(tc.manual_schedule())
+        tp = ctx.enter_context(tc.psum_pool(name="tp", bufs=2))
+        qp = ctx.enter_context(tc.psum_pool(name="qp", bufs=3))
+        accp = ctx.enter_context(tc.psum_pool(name="accp", bufs=3))
+        ctx.enter_context(tc.manual_schedule())
 
         grid_bf = const.tile([P, G], BF16, name="grid_bf")
         nc.sync.dma_start(out=grid_bf[:], in_=grid.partition_broadcast(P))
-        x_first = const.tile([P, SPAN_T, I], BF16, name="x_first")
-        nc.sync.dma_start(out=x_first[:], in_=xv[:, 0:SPAN_T, :])
+        x_sb = []
+        g_sb = []
+
+        def load_x(s):
+            x_t = xpool.tile([P, SPAN_T, I], BF16, name="x_sb", tag="x_sb")
+            nc.sync.dma_start(out=x_t[:], in_=xv[:, s * SPAN_T : (s + 1) * SPAN_T, :])
+            x_sb.append(x_t)
+
+        load_x(0)
         w_a = const.tile([P, 2, O], BF16, name="w_a")
         nc.sync.dma_start(out=w_a[:], in_=wv[:, 0:2, :])
-        g_sb = []
         g_t = gpool.tile([P, SPAN_T, O], BF16, name="g_sb", tag="g_sb")
         g_sb.append(g_t)
         nc.sync.dma_start(out=g_t[:, 0:4, :], in_=gv[:, 0:4, :])
         nc.sync.dma_start(out=g_t[:, 4:8, :], in_=gv[:, 4:8, :])
+        load_x(1)
         w_b = const.tile([P, G - 2, O], BF16, name="w_b")
         nc.sync.dma_start(out=w_b[:], in_=wv[:, 2:G, :])
         wb_raw = const.tile([P, 4, I], BF16, name="wb_raw")
@@ -76,18 +80,15 @@ def tile_rbfkanlayer_t_kernel(tc, x, spline_weight, base_weight, grid, grad_out,
                 out=wb_raw[:, 2 * u : 2 * u + 2, :],
                 in_=base_weight[256 * u : 256 * u + 256, :].rearrange("(p e) c -> p e c", e=2),
             )
-        x_rest = const.tile([P, NT - SPAN_T, I], BF16, name="x_rest")
-        nc.sync.dma_start(out=x_rest[:], in_=xv[:, SPAN_T:NT, :])
         for s in range(1, NSPAN):
             g_t = gpool.tile([P, SPAN_T, O], BF16, name="g_sb", tag="g_sb")
             nc.sync.dma_start(out=g_t[:], in_=gv[:, s * SPAN_T : (s + 1) * SPAN_T, :])
             g_sb.append(g_t)
+            if s + 1 < NSPAN:
+                load_x(s + 1)
 
         def w_rows(g):
             return w_a[:, g, :] if g < 2 else w_b[:, g - 2, :]
-
-        def x_rows(t):
-            return x_first[:, t, :] if t < SPAN_T else x_rest[:, t - SPAN_T, :]
 
         ident_b = const.tile([P, P], BF16, name="ident_b")
         make_identity(nc, ident_b[:])
@@ -116,14 +117,10 @@ def tile_rbfkanlayer_t_kernel(tc, x, spline_weight, base_weight, grid, grad_out,
             nc.vector.tensor_copy(out=dst, in_=ps[:].rearrange("p u n -> p n u"))
 
         def prep_tasks(s):
-            tasks = []
-
             def x_pe():
                 ps = tp.tile([P, SPAN], BF16, name="ps_x", tag="tp")
                 for tt in range(SPAN_T):
-                    nc.tensor.transpose(
-                        out=ps[:, tt * P : (tt + 1) * P], in_=x_rows(s * SPAN_T + tt), identity=ident_b[:]
-                    )
+                    nc.tensor.transpose(out=ps[:, tt * P : (tt + 1) * P], in_=x_sb[s][:, tt, :], identity=ident_b[:])
                 return ps
 
             def x_copy(ps):
@@ -134,12 +131,12 @@ def tile_rbfkanlayer_t_kernel(tc, x, spline_weight, base_weight, grid, grad_out,
                     nc.vector.tensor_copy(out=xt[:], in_=ps[:])
                 xT[s] = xt
 
-            tasks.append((x_pe, x_copy))
             gq = gqpool.tile([P, 4 * SPAN], BF16, name="gq", tag="gq", align_bytes=64)
             gq_f = gq[:].bitcast(F32).rearrange("p (n u) -> p n u", u=2)
             gc = gcpool.tile([P, SPAN], U32, name="gc", tag="gc", align_bytes=64)
             gs = gcpool.tile([P, SPAN], U8, name="gs", tag="gs", align_bytes=64)
             g_codes[s] = (gc, gs)
+            tasks = [(x_pe, x_copy)]
             for b in range(4):
                 tasks.append(
                     (
@@ -148,13 +145,12 @@ def tile_rbfkanlayer_t_kernel(tc, x, spline_weight, base_weight, grid, grad_out,
                     )
                 )
 
-            def quantise():
-                for h in range(2):
-                    nc.vector.quantize_mx(
-                        out=gc[:, h * HALF : (h + 1) * HALF].bitcast(E5X4),
-                        scales=gs[:, h * HALF : (h + 1) * HALF],
-                        in_=gq[:, 4 * h * HALF : 4 * (h + 1) * HALF],
-                    )
+            def quantise(h):
+                nc.vector.quantize_mx(
+                    out=gc[:, h * HALF : (h + 1) * HALF].bitcast(E5X4),
+                    scales=gs[:, h * HALF : (h + 1) * HALF],
+                    in_=gq[:, 4 * h * HALF : 4 * (h + 1) * HALF],
+                )
 
             return tasks, quantise
 
@@ -164,9 +160,7 @@ def tile_rbfkanlayer_t_kernel(tc, x, spline_weight, base_weight, grid, grad_out,
         wq_f = wq[:, 0 : 4 * G * I].bitcast(F32).rearrange("p (n u) -> p n u", u=2)
 
         def w_quant(c0, c1):
-            nc.vector.quantize_mx(
-                out=wc[:, c0:c1].bitcast(E4X4), scales=ws[:, c0:c1], in_=wq[:, 4 * c0 : 4 * c1]
-            )
+            nc.vector.quantize_mx(out=wc[:, c0:c1].bitcast(E4X4), scales=ws[:, c0:c1], in_=wq[:, 4 * c0 : 4 * c1])
 
         def w_pairs(pairs):
             for b in pairs:
@@ -184,17 +178,16 @@ def tile_rbfkanlayer_t_kernel(tc, x, spline_weight, base_weight, grid, grad_out,
         first, first_quantise = prep_tasks(0)
         first[0][1](first[0][0]())
         w_pairs([0])
-        for pe_part, v_part in first[1:]:
+        for b in range(4):
+            pe_part, v_part = first[1 + b]
             v_part(pe_part())
-        first_quantise()
+            if b % 2 == 1:
+                first_quantise(b // 2)
         head_rest = [lambda: w_pairs([1]), lambda: w_pairs([2, 3]), w_base]
 
-        NU = NSPAN * NJ
-        NB = 2 * NU
         e_of = {}
         q_of = {}
         r_of = {}
-        acc_of = {}
 
         def emit_scalar(k):
             if k >= NU:
@@ -225,6 +218,19 @@ def tile_rbfkanlayer_t_kernel(tc, x, spline_weight, base_weight, grid, grad_out,
             )
             q_of[n] = q
 
+        def add_transposed(src, acc, first_one, last_one):
+            for tt in range(SPAN_T):
+                nc.tensor.matmul(
+                    out=acc[tt // 4][:, (tt % 4) * P : (tt % 4 + 1) * P],
+                    lhsT=src[:, tt * P : (tt + 1) * P],
+                    rhs=ident_f[:],
+                    is_transpose=True,
+                    start=(first_one and tt % 4 == 0),
+                    stop=(last_one and tt % 4 == 3),
+                )
+
+        acc_of = {}
+
         def emit_evac(n):
             k, h = n // 2, n % 2
             s, g = k // NJ, k % NJ
@@ -250,25 +256,31 @@ def tile_rbfkanlayer_t_kernel(tc, x, spline_weight, base_weight, grid, grad_out,
             s, j = k // NJ, k % NJ
             if j == 0:
                 acc_of[s] = [accp.tile([P, HALF], F32, name="acc%d" % h, tag="acc") for h in range(2)]
-            for tt in range(SPAN_T):
-                nc.tensor.matmul(
-                    out=acc_of[s][tt // 4][:, (tt % 4) * P : (tt % 4 + 1) * P],
-                    lhsT=r_of[k][:, tt * P : (tt + 1) * P],
-                    rhs=ident_f[:],
-                    is_transpose=True,
-                    start=(j == 0 and tt % 4 == 0),
-                    stop=(j == NJ - 1 and tt % 4 == 3),
-                )
+            last_j = G - 1 if s == NSPAN - 1 else G
+            add_transposed(r_of[k], acc_of[s], j == 0, j == last_j)
 
         def emit_out(s):
             o_sb = opool.tile([P, SPAN_T, I], F32, name="o_sb", tag="o_sb")
+            last_span = s == NSPAN - 1
             for h in range(2):
                 dst = o_sb[:, 4 * h : 4 * h + 4, :].rearrange("p t i -> p (t i)")
-                if OUT_ON_SCALAR and s + 1 < NSPAN:
+                if (OUT_ON_SCALAR and not last_span) or (last_span and h == 0):
                     nc.scalar.activation(out=dst, in_=acc_of[s][h][:], func=ACT.Copy, scale=-40.0)
                 else:
                     nc.vector.tensor_scalar_mul(out=dst, in0=acc_of[s][h][:], scalar1=-40.0)
-            nc.sync.dma_start(out=ov[:, s * SPAN_T : (s + 1) * SPAN_T, :], in_=o_sb[:])
+                if last_span:
+                    t0 = s * SPAN_T + 4 * h
+                    nc.sync.dma_start(out=ov[:, t0 : t0 + 4, :], in_=o_sb[:, 4 * h : 4 * h + 4, :])
+            if not last_span:
+                nc.sync.dma_start(out=ov[:, s * SPAN_T : (s + 1) * SPAN_T, :], in_=o_sb[:])
+
+        def vector_window(s, quantise_next):
+            if quantise_next is not None:
+                quantise_next(0)
+                quantise_next(1)
+            for jj in range(N_GPSIMD, G):
+                emit_mult(nc.vector, s * NJ + jj)
+                emit_acc(s * NJ + jj)
 
         for k in range(S_AHEAD):
             emit_scalar(k)
@@ -285,15 +297,12 @@ def tile_rbfkanlayer_t_kernel(tc, x, spline_weight, base_weight, grid, grad_out,
             s, j = k // NJ, k % NJ
             if h == 0:
                 emit_scalar(k + S_AHEAD)
-                if j == 0 and s + 1 < NSPAN:
-                    tasks, quantise_next = prep_tasks(s + 1)
-                    task_i = 0
-            if j == G and h == 0:
-                if s + 1 < NSPAN:
-                    quantise_next()
-                for jj in range(N_GPSIMD, G):
-                    emit_mult(nc.vector, s * NJ + jj)
-                    emit_acc(s * NJ + jj)
+                if j == 0:
+                    tasks, quantise_next, task_i = [], None, 0
+                    if s + 1 < NSPAN:
+                        tasks, quantise_next = prep_tasks(s + 1)
+            if j == G and h == 0 and s + 1 < NSPAN:
+                vector_window(s, quantise_next)
             emit_mx(n + 2)
             if h == 1 and j < G:
                 if 0 <= j - LAG < N_GPSIMD:
@@ -322,4 +331,5 @@ def tile_rbfkanlayer_t_kernel(tc, x, spline_weight, base_weight, grid, grad_out,
                 if j == 0 and out_pending >= 0:
                     emit_out(out_pending)
                     out_pending = -1
-        emit_out(out_pending)
+        vector_window(NSPAN - 1, None)
+        emit_out(NSPAN - 1)

@@ -27,9 +27,10 @@ LAG = 3
 S_AHEAD = 4
 E_BUFS = 8
 R_BUFS = 8
-N_GPSIMD = 4
+OUT_AT = 1
+N_GPSIMD = 5
 OUT_ON_SCALAR = True
-XT_ON_SCALAR = True
+XT_ON_SCALAR = False
 
 
 def tile_rbfkanlayer_t_kernel(tc, x, spline_weight, base_weight, grid, grad_out, out):
@@ -256,8 +257,7 @@ def tile_rbfkanlayer_t_kernel(tc, x, spline_weight, base_weight, grid, grad_out,
             s, j = k // NJ, k % NJ
             if j == 0:
                 acc_of[s] = [accp.tile([P, HALF], F32, name="acc%d" % h, tag="acc") for h in range(2)]
-            last_j = G - 1 if s == NSPAN - 1 else G
-            add_transposed(r_of[k], acc_of[s], j == 0, j == last_j)
+            add_transposed(r_of[k], acc_of[s], j == 0, j == G - 1)
 
         def emit_out(s):
             o_sb = opool.tile([P, SPAN_T, I], F32, name="o_sb", tag="o_sb")
@@ -278,6 +278,9 @@ def tile_rbfkanlayer_t_kernel(tc, x, spline_weight, base_weight, grid, grad_out,
             if quantise_next is not None:
                 quantise_next(0)
                 quantise_next(1)
+                emit_mx(2 * (s + 1) * NJ)
+                emit_mx(2 * (s + 1) * NJ + 1)
+            emit_acc(s * NJ + G)
             for jj in range(N_GPSIMD, G):
                 emit_mult(nc.vector, s * NJ + jj)
                 emit_acc(s * NJ + jj)
@@ -301,9 +304,8 @@ def tile_rbfkanlayer_t_kernel(tc, x, spline_weight, base_weight, grid, grad_out,
                     tasks, quantise_next, task_i = [], None, 0
                     if s + 1 < NSPAN:
                         tasks, quantise_next = prep_tasks(s + 1)
-            if j == G and h == 0 and s + 1 < NSPAN:
-                vector_window(s, quantise_next)
-            emit_mx(n + 2)
+            if j < G:
+                emit_mx(n + 2)
             if h == 1 and j < G:
                 if 0 <= j - LAG < N_GPSIMD:
                     emit_acc(s * NJ + j - LAG)
@@ -326,10 +328,9 @@ def tile_rbfkanlayer_t_kernel(tc, x, spline_weight, base_weight, grid, grad_out,
                 if j < N_GPSIMD:
                     emit_mult(nc.gpsimd, k)
                 if j == G:
-                    emit_acc(k)
+                    vector_window(s, quantise_next)
                     out_pending = s
-                if j == 0 and out_pending >= 0:
+                if j == OUT_AT and out_pending >= 0:
                     emit_out(out_pending)
                     out_pending = -1
-        vector_window(NSPAN - 1, None)
         emit_out(NSPAN - 1)

@@ -53,7 +53,6 @@ def tile_rbfkanlayer_t_kernel(tc, x, spline_weight, base_weight, grid, grad_out,
         tp = ctx.enter_context(tc.psum_pool(name="tp", bufs=2))
         qp = ctx.enter_context(tc.psum_pool(name="qp", bufs=3))
         accp = ctx.enter_context(tc.psum_pool(name="accp", bufs=3))
-        ctx.enter_context(tc.manual_schedule())
 
         grid_bf = const.tile([P, G], BF16, name="grid_bf")
         nc.sync.dma_start(out=grid_bf[:], in_=grid.partition_broadcast(P))

@@ -27,10 +27,6 @@ LAG = 3
 S_AHEAD = 4
 E_BUFS = 8
 R_BUFS = 8
-OUT_AT = 1
-N_GPSIMD = 5
-OUT_ON_SCALAR = True
-XT_ON_SCALAR = False
 
 
 def tile_rbfkanlayer_t_kernel(tc, x, spline_weight, base_weight, grid, grad_out, out):
@@ -125,10 +121,7 @@ def tile_rbfkanlayer_t_kernel(tc, x, spline_weight, base_weight, grid, grad_out,
 
             def x_copy(ps):
                 xt = xtpool.tile([P, SPAN], BF16, name="xT", tag="xT")
-                if XT_ON_SCALAR and s > 0:
-                    nc.scalar.copy(out=xt[:], in_=ps[:])
-                else:
-                    nc.vector.tensor_copy(out=xt[:], in_=ps[:])
+                nc.vector.tensor_copy(out=xt[:], in_=ps[:])
                 xT[s] = xt
 
             gq = gqpool.tile([P, 4 * SPAN], BF16, name="gq", tag="gq", align_bytes=64)
@@ -145,12 +138,8 @@ def tile_rbfkanlayer_t_kernel(tc, x, spline_weight, base_weight, grid, grad_out,
                     )
                 )
 
-            def quantise(h):
-                nc.vector.quantize_mx(
-                    out=gc[:, h * HALF : (h + 1) * HALF].bitcast(E5X4),
-                    scales=gs[:, h * HALF : (h + 1) * HALF],
-                    in_=gq[:, 4 * h * HALF : 4 * (h + 1) * HALF],
-                )
+            def quantise(c0, c1):
+                nc.vector.quantize_mx(out=gc[:, c0:c1].bitcast(E5X4), scales=gs[:, c0:c1], in_=gq[:, 4 * c0 : 4 * c1])
 
             return tasks, quantise
 
@@ -182,7 +171,7 @@ def tile_rbfkanlayer_t_kernel(tc, x, spline_weight, base_weight, grid, grad_out,
             pe_part, v_part = first[1 + b]
             v_part(pe_part())
             if b % 2 == 1:
-                first_quantise(b // 2)
+                first_quantise(b // 2 * HALF, (b // 2 + 1) * HALF)
         head_rest = [lambda: w_pairs([1]), lambda: w_pairs([2, 3]), w_base]
 
         e_of = {}
@@ -249,21 +238,21 @@ def tile_rbfkanlayer_t_kernel(tc, x, spline_weight, base_weight, grid, grad_out,
             else:
                 nc.vector.tensor_scalar_mul(out=r[:, h * HALF : (h + 1) * HALF], in0=q_of[n][:], scalar1=-1.0 / 40.0)
 
-        def emit_mult(eng, k):
-            eng.tensor_tensor(out=r_of[k][:], in0=r_of[k][:], in1=e_of[k][:], op=ALU.mult)
-
-        def emit_acc(k):
-            s, j = k // NJ, k % NJ
-            if j == 0:
-                acc_of[s] = [accp.tile([P, HALF], F32, name="acc%d" % h, tag="acc") for h in range(2)]
-            add_transposed(r_of[k], acc_of[s], j == 0, j == G - 1)
+        def emit_mult(k):
+            s, g = k // NJ, k % NJ
+            if s == NSPAN - 1 and g == G - 1:
+                for h in range(2):
+                    part = slice(h * HALF, (h + 1) * HALF)
+                    nc.vector.tensor_tensor(out=r_of[k][:, part], in0=r_of[k][:, part], in1=e_of[k][:, part], op=ALU.mult)
+            else:
+                nc.gpsimd.tensor_tensor(out=r_of[k][:], in0=r_of[k][:], in1=e_of[k][:], op=ALU.mult)
 
         def emit_out(s):
             o_sb = opool.tile([P, SPAN_T, I], F32, name="o_sb", tag="o_sb")
             last_span = s == NSPAN - 1
             for h in range(2):
                 dst = o_sb[:, 4 * h : 4 * h + 4, :].rearrange("p t i -> p (t i)")
-                if (OUT_ON_SCALAR and not last_span) or (last_span and h == 0):
+                if last_span and h == 0:
                     nc.scalar.activation(out=dst, in_=acc_of[s][h][:], func=ACT.Copy, scale=-40.0)
                 else:
                     nc.vector.tensor_scalar_mul(out=dst, in0=acc_of[s][h][:], scalar1=-40.0)
@@ -273,16 +262,15 @@ def tile_rbfkanlayer_t_kernel(tc, x, spline_weight, base_weight, grid, grad_out,
             if not last_span:
                 nc.sync.dma_start(out=ov[:, s * SPAN_T : (s + 1) * SPAN_T, :], in_=o_sb[:])
 
-        def vector_window(s, quantise_next):
-            if quantise_next is not None:
-                quantise_next(0)
-                quantise_next(1)
-                emit_mx(2 * (s + 1) * NJ)
-                emit_mx(2 * (s + 1) * NJ + 1)
-            emit_acc(s * NJ + G)
-            for jj in range(N_GPSIMD, G):
-                emit_mult(nc.vector, s * NJ + jj)
-                emit_acc(s * NJ + jj)
+        acc_order = list(range(G - 2)) + [G, G - 2, G - 1]
+
+        def emit_acc(a):
+            s, j = a // NJ, acc_order[a % NJ]
+            if a % NJ == 0:
+                acc_of[s] = [accp.tile([P, HALF], F32, name="acc%d" % h, tag="acc") for h in range(2)]
+            add_transposed(r_of[s * NJ + j], acc_of[s], a % NJ == 0, a % NJ == NJ - 1)
+            if a % NJ == NJ - 1:
+                emit_out(s)
 
         for k in range(S_AHEAD):
             emit_scalar(k)
@@ -293,7 +281,6 @@ def tile_rbfkanlayer_t_kernel(tc, x, spline_weight, base_weight, grid, grad_out,
         task_i = 0
         head_i = 0
         pending = None
-        out_pending = -1
         for n in range(NB):
             k, h = n // 2, n % 2
             s, j = k // NJ, k % NJ
@@ -303,19 +290,14 @@ def tile_rbfkanlayer_t_kernel(tc, x, spline_weight, base_weight, grid, grad_out,
                     tasks, quantise_next, task_i = [], None, 0
                     if s + 1 < NSPAN:
                         tasks, quantise_next = prep_tasks(s + 1)
-            if j < G:
-                emit_mx(n + 2)
-            if h == 1 and j < G:
-                if 0 <= j - LAG < N_GPSIMD:
-                    emit_acc(s * NJ + j - LAG)
-                if j == G - 1:
-                    for z in range(max(0, G - LAG), N_GPSIMD):
-                        emit_acc(s * NJ + z)
+            if h == 1 and k >= LAG:
+                emit_acc(k - LAG)
             fresh = None
             if h == 1 and j < G and task_i < len(tasks):
                 pe_part, v_part = tasks[task_i]
                 task_i += 1
                 fresh = (v_part, pe_part())
+            emit_mx(n + 2)
             emit_evac(n)
             if h == 1:
                 if pending is not None:
@@ -324,12 +306,9 @@ def tile_rbfkanlayer_t_kernel(tc, x, spline_weight, base_weight, grid, grad_out,
                 if head_i < len(head_rest):
                     head_rest[head_i]()
                     head_i += 1
-                if j < N_GPSIMD:
-                    emit_mult(nc.gpsimd, k)
-                if j == G:
-                    vector_window(s, quantise_next)
-                    out_pending = s
-                if j == OUT_AT and out_pending >= 0:
-                    emit_out(out_pending)
-                    out_pending = -1
-        emit_out(NSPAN - 1)
+                if j < G:
+                    emit_mult(k)
+                if j == 6 and quantise_next is not None:
+                    quantise_next(0, SPAN)
+        for a in range(NU - LAG, NU):
+            emit_acc(a)

@@ -23,10 +23,12 @@ NJ = G + 1
 NU = NSPAN * NJ
 NB = 2 * NU
 FLOPS = 2 * B * O * (I + I * G)
-LAG = 3
+LAG = 4
 S_AHEAD = 4
 E_BUFS = 8
-R_BUFS = 8
+R_BUFS = 9
+N_VECTOR = 2
+X_TASK = 3
 
 
 def tile_rbfkanlayer_t_kernel(tc, x, spline_weight, base_weight, grid, grad_out, out):
@@ -47,8 +49,9 @@ def tile_rbfkanlayer_t_kernel(tc, x, spline_weight, base_weight, grid, grad_out,
         rpool = ctx.enter_context(tc.tile_pool(name="rpool", bufs=R_BUFS))
         opool = ctx.enter_context(tc.tile_pool(name="opool", bufs=2))
         tp = ctx.enter_context(tc.psum_pool(name="tp", bufs=2))
+        xp = ctx.enter_context(tc.psum_pool(name="xp", bufs=1))
         qp = ctx.enter_context(tc.psum_pool(name="qp", bufs=3))
-        accp = ctx.enter_context(tc.psum_pool(name="accp", bufs=3))
+        accp = ctx.enter_context(tc.psum_pool(name="accp", bufs=2))
 
         grid_bf = const.tile([P, G], BF16, name="grid_bf")
         nc.sync.dma_start(out=grid_bf[:], in_=grid.partition_broadcast(P))
@@ -96,6 +99,7 @@ def tile_rbfkanlayer_t_kernel(tc, x, spline_weight, base_weight, grid, grad_out,
         nc.vector.tensor_scalar_mul(out=c_neg[:], in0=grid_bf[:], scalar1=-1.0)
 
         xT = {}
+        xT_ps = {}
         g_codes = {}
 
         def words_pe(src0, src1):
@@ -114,7 +118,7 @@ def tile_rbfkanlayer_t_kernel(tc, x, spline_weight, base_weight, grid, grad_out,
 
         def prep_tasks(s):
             def x_pe():
-                ps = tp.tile([P, SPAN], BF16, name="ps_x", tag="tp")
+                ps = xp.tile([P, SPAN], BF16, name="ps_x", tag="xp")
                 for tt in range(SPAN_T):
                     nc.tensor.transpose(out=ps[:, tt * P : (tt + 1) * P], in_=x_sb[s][:, tt, :], identity=ident_b[:])
                 return ps
@@ -123,13 +127,14 @@ def tile_rbfkanlayer_t_kernel(tc, x, spline_weight, base_weight, grid, grad_out,
                 xt = xtpool.tile([P, SPAN], BF16, name="xT", tag="xT")
                 nc.vector.tensor_copy(out=xt[:], in_=ps[:])
                 xT[s] = xt
+                xT_ps[s] = ps
 
             gq = gqpool.tile([P, 4 * SPAN], BF16, name="gq", tag="gq", align_bytes=64)
             gq_f = gq[:].bitcast(F32).rearrange("p (n u) -> p n u", u=2)
             gc = gcpool.tile([P, SPAN], U32, name="gc", tag="gc", align_bytes=64)
             gs = gcpool.tile([P, SPAN], U8, name="gs", tag="gs", align_bytes=64)
             g_codes[s] = (gc, gs)
-            tasks = [(x_pe, x_copy)]
+            tasks = []
             for b in range(4):
                 tasks.append(
                     (
@@ -137,6 +142,8 @@ def tile_rbfkanlayer_t_kernel(tc, x, spline_weight, base_weight, grid, grad_out,
                         lambda ps, b=b: words_copy(ps, gq_f[:, 2 * P * b : 2 * P * (b + 1), :]),
                     )
                 )
+
+            tasks.insert(X_TASK, (x_pe, x_copy))
 
             def quantise(c0, c1):
                 nc.vector.quantize_mx(out=gc[:, c0:c1].bitcast(E5X4), scales=gs[:, c0:c1], in_=gq[:, 4 * c0 : 4 * c1])
@@ -165,10 +172,11 @@ def tile_rbfkanlayer_t_kernel(tc, x, spline_weight, base_weight, grid, grad_out,
             w_quant(G * I, NJ * I)
 
         first, first_quantise = prep_tasks(0)
-        first[0][1](first[0][0]())
+        x_pe, x_copy = first.pop(X_TASK)
+        x_copy(x_pe())
         w_pairs([0])
         for b in range(4):
-            pe_part, v_part = first[1 + b]
+            pe_part, v_part = first[b]
             v_part(pe_part())
             if b % 2 == 1:
                 first_quantise(b // 2 * HALF, (b // 2 + 1) * HALF)
@@ -226,7 +234,14 @@ def tile_rbfkanlayer_t_kernel(tc, x, spline_weight, base_weight, grid, grad_out,
             if h == 0:
                 r_of[k] = rpool.tile([P, SPAN], F32, name="r", tag="r")
             r = r_of[k]
-            if g < G:
+            if g < N_VECTOR:
+                nc.vector.tensor_tensor(
+                    out=r[:, h * HALF : (h + 1) * HALF],
+                    in0=q_of[n][:],
+                    in1=e_of[k][:, h * HALF : (h + 1) * HALF],
+                    op=ALU.mult,
+                )
+            elif g < G:
                 nc.vector.scalar_tensor_tensor(
                     out=r[:, h * HALF : (h + 1) * HALF],
                     in0=xT[s][:, h * HALF : (h + 1) * HALF],
@@ -240,7 +255,11 @@ def tile_rbfkanlayer_t_kernel(tc, x, spline_weight, base_weight, grid, grad_out,
 
         def emit_mult(k):
             s, g = k // NJ, k % NJ
-            if s == NSPAN - 1 and g == G - 1:
+            if g < N_VECTOR:
+                nc.vector.scalar_tensor_tensor(
+                    out=r_of[k][:], in0=xT_ps[s][:], scalar=c_pos[:, g : g + 1], in1=r_of[k][:], op0=ALU.subtract, op1=ALU.mult
+                )
+            elif s == NSPAN - 1 and g == G - 1:
                 for h in range(2):
                     part = slice(h * HALF, (h + 1) * HALF)
                     nc.vector.tensor_tensor(out=r_of[k][:, part], in0=r_of[k][:, part], in1=e_of[k][:, part], op=ALU.mult)
@@ -269,8 +288,6 @@ def tile_rbfkanlayer_t_kernel(tc, x, spline_weight, base_weight, grid, grad_out,
             if a % NJ == 0:
                 acc_of[s] = [accp.tile([P, HALF], F32, name="acc%d" % h, tag="acc") for h in range(2)]
             add_transposed(r_of[s * NJ + j], acc_of[s], a % NJ == 0, a % NJ == NJ - 1)
-            if a % NJ == NJ - 1:
-                emit_out(s)
 
         for k in range(S_AHEAD):
             emit_scalar(k)
@@ -290,6 +307,8 @@ def tile_rbfkanlayer_t_kernel(tc, x, spline_weight, base_weight, grid, grad_out,
                     tasks, quantise_next, task_i = [], None, 0
                     if s + 1 < NSPAN:
                         tasks, quantise_next = prep_tasks(s + 1)
+            if h == 0 and k > LAG and (k - LAG) % NJ == 0:
+                emit_out((k - LAG) // NJ - 1)
             if h == 1 and k >= LAG:
                 emit_acc(k - LAG)
             fresh = None
@@ -306,9 +325,12 @@ def tile_rbfkanlayer_t_kernel(tc, x, spline_weight, base_weight, grid, grad_out,
                 if head_i < len(head_rest):
                     head_rest[head_i]()
                     head_i += 1
-                if j < G:
+                if N_VECTOR <= j < G:
                     emit_mult(k)
+                if 1 <= j <= N_VECTOR:
+                    emit_mult(k - 1)
                 if j == 6 and quantise_next is not None:
                     quantise_next(0, SPAN)
         for a in range(NU - LAG, NU):
             emit_acc(a)
+        emit_out(NSPAN - 1)

@@ -23,7 +23,10 @@ NJ = G + 1
 NU = NSPAN * NJ
 NB = 2 * NU
 FLOPS = 2 * B * O * (I + I * G)
-LAG = 4
+BASE = 8
+STEPS = [0, 1, 2, BASE, 3, 4, 5, 6, 7]
+SUMS = {6: [0], 7: [1], 8: [2, 3], 9: [4], 10: [5], 11: [6], 13: [7]}
+OUT_STEP = 14
 S_AHEAD = 4
 E_BUFS = 8
 R_BUFS = 9
@@ -66,6 +69,12 @@ def tile_rbfkanlayer_t_kernel(tc, x, spline_weight, base_weight, grid, grad_out,
         load_x(0)
         w_a = const.tile([P, 2, O], BF16, name="w_a")
         nc.sync.dma_start(out=w_a[:], in_=wv[:, 0:2, :])
+        wb_raw = const.tile([P, 4, I], BF16, name="wb_raw")
+        for u in range(2):
+            nc.sync.dma_start(
+                out=wb_raw[:, 2 * u : 2 * u + 2, :],
+                in_=base_weight[256 * u : 256 * u + 256, :].rearrange("(p e) c -> p e c", e=2),
+            )
         g_t = gpool.tile([P, SPAN_T, O], BF16, name="g_sb", tag="g_sb")
         g_sb.append(g_t)
         nc.sync.dma_start(out=g_t[:, 0:4, :], in_=gv[:, 0:4, :])
@@ -73,12 +82,6 @@ def tile_rbfkanlayer_t_kernel(tc, x, spline_weight, base_weight, grid, grad_out,
         load_x(1)
         w_b = const.tile([P, G - 2, O], BF16, name="w_b")
         nc.sync.dma_start(out=w_b[:], in_=wv[:, 2:G, :])
-        wb_raw = const.tile([P, 4, I], BF16, name="wb_raw")
-        for u in range(2):
-            nc.sync.dma_start(
-                out=wb_raw[:, 2 * u : 2 * u + 2, :],
-                in_=base_weight[256 * u : 256 * u + 256, :].rearrange("(p e) c -> p e c", e=2),
-            )
         for s in range(1, NSPAN):
             g_t = gpool.tile([P, SPAN_T, O], BF16, name="g_sb", tag="g_sb")
             nc.sync.dma_start(out=g_t[:], in_=gv[:, s * SPAN_T : (s + 1) * SPAN_T, :])
@@ -113,20 +116,24 @@ def tile_rbfkanlayer_t_kernel(tc, x, spline_weight, base_weight, grid, grad_out,
                     )
             return ps
 
+        def x_transposed(s, pool, tag):
+            ps = pool.tile([P, SPAN], BF16, name="ps_x", tag=tag)
+            for tt in range(SPAN_T):
+                nc.tensor.transpose(out=ps[:, tt * P : (tt + 1) * P], in_=x_sb[s][:, tt, :], identity=ident_b[:])
+            return ps
+
         def words_copy(ps, dst):
             nc.vector.tensor_copy(out=dst, in_=ps[:].rearrange("p u n -> p n u"))
 
         def prep_tasks(s):
             def x_pe():
-                ps = xp.tile([P, SPAN], BF16, name="ps_x", tag="xp")
-                for tt in range(SPAN_T):
-                    nc.tensor.transpose(out=ps[:, tt * P : (tt + 1) * P], in_=x_sb[s][:, tt, :], identity=ident_b[:])
-                return ps
+                return x_transposed(s, xp, "xp")
 
             def x_copy(ps):
-                xt = xtpool.tile([P, SPAN], BF16, name="xT", tag="xT")
-                nc.vector.tensor_copy(out=xt[:], in_=ps[:])
-                xT[s] = xt
+                if s not in xT:
+                    xt = xtpool.tile([P, SPAN], BF16, name="xT", tag="xT")
+                    nc.vector.tensor_copy(out=xt[:], in_=ps[:])
+                    xT[s] = xt
                 xT_ps[s] = ps
 
             gq = gqpool.tile([P, 4 * SPAN], BF16, name="gq", tag="gq", align_bytes=64)
@@ -180,28 +187,38 @@ def tile_rbfkanlayer_t_kernel(tc, x, spline_weight, base_weight, grid, grad_out,
             v_part(pe_part())
             if b % 2 == 1:
                 first_quantise(b // 2 * HALF, (b // 2 + 1) * HALF)
-        head_rest = [lambda: w_pairs([1]), lambda: w_pairs([2, 3]), w_base]
+
+        def x_second():
+            ps = x_transposed(1, tp, "tp")
+            xt = xtpool.tile([P, SPAN], BF16, name="xT", tag="xT")
+            nc.vector.tensor_copy(out=xt[:], in_=ps[:])
+            xT[1] = xt
+
+        head_rest = [lambda: w_pairs([1]), w_base, x_second, lambda: w_pairs([2, 3])]
 
         e_of = {}
         q_of = {}
         r_of = {}
 
+        def unit(k):
+            return k // NJ, STEPS[k % NJ]
+
         def emit_scalar(k):
             if k >= NU:
                 return
-            s, g = k // NJ, k % NJ
-            if g == G:
+            s, g = unit(k)
+            if g == BASE:
                 return
             e = epool.tile([P, SPAN], F32, name="e", tag="e")
-            e_of[k] = e
+            e_of[s, g] = e
             nc.scalar.activation(out=e[:], in_=xT[s][:], func=ACT.Square, bias=c_neg[:, g : g + 1], scale=1.0)
             nc.scalar.activation(out=e[:], in_=e[:], func=ACT.Exp, scale=-20.0)
 
         def emit_mx(n):
             if n >= NB:
                 return
-            k, h = n // 2, n % 2
-            s, g = k // NJ, k % NJ
+            h = n % 2
+            s, g = unit(n // 2)
             gc, gs = g_codes[s]
             q = qp.tile([P, HALF], F32, name="q", tag="q")
             nc.tensor.matmul_mx(
@@ -215,63 +232,64 @@ def tile_rbfkanlayer_t_kernel(tc, x, spline_weight, base_weight, grid, grad_out,
             )
             q_of[n] = q
 
-        def add_transposed(src, acc, first_one, last_one):
-            for tt in range(SPAN_T):
-                nc.tensor.matmul(
-                    out=acc[tt // 4][:, (tt % 4) * P : (tt % 4 + 1) * P],
-                    lhsT=src[:, tt * P : (tt + 1) * P],
-                    rhs=ident_f[:],
-                    is_transpose=True,
-                    start=(first_one and tt % 4 == 0),
-                    stop=(last_one and tt % 4 == 3),
-                )
-
         acc_of = {}
 
-        def emit_evac(n):
-            k, h = n // 2, n % 2
-            s, g = k // NJ, k % NJ
-            if h == 0:
-                r_of[k] = rpool.tile([P, SPAN], F32, name="r", tag="r")
-            r = r_of[k]
-            if g < N_VECTOR:
-                nc.vector.tensor_tensor(
-                    out=r[:, h * HALF : (h + 1) * HALF],
-                    in0=q_of[n][:],
-                    in1=e_of[k][:, h * HALF : (h + 1) * HALF],
-                    op=ALU.mult,
+        def emit_sum(s, g):
+            if g == 0:
+                acc_of[s] = [accp.tile([P, HALF], F32, name="acc%d" % h, tag="acc") for h in range(2)]
+            for tt in range(SPAN_T):
+                nc.tensor.matmul(
+                    out=acc_of[s][tt // 4][:, (tt % 4) * P : (tt % 4 + 1) * P],
+                    lhsT=r_of[s, g][:, tt * P : (tt + 1) * P],
+                    rhs=ident_f[:],
+                    is_transpose=True,
+                    start=(g == 0 and tt % 4 == 0),
+                    stop=(g == G - 1 and tt % 4 == 3),
                 )
-            elif g < G:
+
+        def emit_evac(n):
+            s, g = unit(n // 2)
+            part = slice(n % 2 * HALF, (n % 2 + 1) * HALF)
+            if g == BASE:
+                r = r_of[s, N_VECTOR - 1]
                 nc.vector.scalar_tensor_tensor(
-                    out=r[:, h * HALF : (h + 1) * HALF],
-                    in0=xT[s][:, h * HALF : (h + 1) * HALF],
+                    out=r[:, part], in0=q_of[n][:], scalar=-1.0 / 40.0, in1=r[:, part], op0=ALU.mult, op1=ALU.add
+                )
+                return
+            if n % 2 == 0:
+                r_of[s, g] = rpool.tile([P, SPAN], F32, name="r", tag="r")
+            r = r_of[s, g]
+            if g < N_VECTOR:
+                nc.vector.tensor_tensor(out=r[:, part], in0=q_of[n][:], in1=e_of[s, g][:, part], op=ALU.mult)
+            else:
+                nc.vector.scalar_tensor_tensor(
+                    out=r[:, part],
+                    in0=xT[s][:, part],
                     scalar=c_pos[:, g : g + 1],
                     in1=q_of[n][:],
                     op0=ALU.subtract,
                     op1=ALU.mult,
                 )
-            else:
-                nc.vector.tensor_scalar_mul(out=r[:, h * HALF : (h + 1) * HALF], in0=q_of[n][:], scalar1=-1.0 / 40.0)
 
-        def emit_mult(k):
-            s, g = k // NJ, k % NJ
+        def emit_mult(s, g):
+            r = r_of[s, g]
             if g < N_VECTOR:
                 nc.vector.scalar_tensor_tensor(
-                    out=r_of[k][:], in0=xT_ps[s][:], scalar=c_pos[:, g : g + 1], in1=r_of[k][:], op0=ALU.subtract, op1=ALU.mult
+                    out=r[:], in0=xT_ps[s][:], scalar=c_pos[:, g : g + 1], in1=r[:], op0=ALU.subtract, op1=ALU.mult
                 )
             elif s == NSPAN - 1 and g == G - 1:
                 for h in range(2):
                     part = slice(h * HALF, (h + 1) * HALF)
-                    nc.vector.tensor_tensor(out=r_of[k][:, part], in0=r_of[k][:, part], in1=e_of[k][:, part], op=ALU.mult)
+                    nc.vector.tensor_tensor(out=r[:, part], in0=r[:, part], in1=e_of[s, g][:, part], op=ALU.mult)
             else:
-                nc.gpsimd.tensor_tensor(out=r_of[k][:], in0=r_of[k][:], in1=e_of[k][:], op=ALU.mult)
+                nc.gpsimd.tensor_tensor(out=r[:], in0=r[:], in1=e_of[s, g][:], op=ALU.mult)
 
         def emit_out(s):
             o_sb = opool.tile([P, SPAN_T, I], F32, name="o_sb", tag="o_sb")
             last_span = s == NSPAN - 1
             for h in range(2):
                 dst = o_sb[:, 4 * h : 4 * h + 4, :].rearrange("p t i -> p (t i)")
-                if last_span and h == 0:
+                if h == 0:
                     nc.scalar.activation(out=dst, in_=acc_of[s][h][:], func=ACT.Copy, scale=-40.0)
                 else:
                     nc.vector.tensor_scalar_mul(out=dst, in0=acc_of[s][h][:], scalar1=-40.0)
@@ -281,13 +299,12 @@ def tile_rbfkanlayer_t_kernel(tc, x, spline_weight, base_weight, grid, grad_out,
             if not last_span:
                 nc.sync.dma_start(out=ov[:, s * SPAN_T : (s + 1) * SPAN_T, :], in_=o_sb[:])
 
-        acc_order = list(range(G - 2)) + [G, G - 2, G - 1]
-
-        def emit_acc(a):
-            s, j = a // NJ, acc_order[a % NJ]
-            if a % NJ == 0:
-                acc_of[s] = [accp.tile([P, HALF], F32, name="acc%d" % h, tag="acc") for h in range(2)]
-            add_transposed(r_of[s * NJ + j], acc_of[s], a % NJ == 0, a % NJ == NJ - 1)
+        def emit_sums(s, step):
+            if s >= 0:
+                for g in SUMS.get(step, []):
+                    emit_sum(s, g)
+                if step == OUT_STEP:
+                    emit_out(s)
 
         for k in range(S_AHEAD):
             emit_scalar(k)
@@ -301,18 +318,18 @@ def tile_rbfkanlayer_t_kernel(tc, x, spline_weight, base_weight, grid, grad_out,
         for n in range(NB):
             k, h = n // 2, n % 2
             s, j = k // NJ, k % NJ
+            g = STEPS[j]
             if h == 0:
                 emit_scalar(k + S_AHEAD)
                 if j == 0:
                     tasks, quantise_next, task_i = [], None, 0
                     if s + 1 < NSPAN:
                         tasks, quantise_next = prep_tasks(s + 1)
-            if h == 0 and k > LAG and (k - LAG) % NJ == 0:
-                emit_out((k - LAG) // NJ - 1)
-            if h == 1 and k >= LAG:
-                emit_acc(k - LAG)
+            else:
+                emit_sums(s - 1, NJ + j)
+                emit_sums(s, j)
             fresh = None
-            if h == 1 and j < G and task_i < len(tasks):
+            if h == 1 and task_i < len(tasks):
                 pe_part, v_part = tasks[task_i]
                 task_i += 1
                 fresh = (v_part, pe_part())
@@ -325,12 +342,11 @@ def tile_rbfkanlayer_t_kernel(tc, x, spline_weight, base_weight, grid, grad_out,
                 if head_i < len(head_rest):
                     head_rest[head_i]()
                     head_i += 1
-                if N_VECTOR <= j < G:
-                    emit_mult(k)
+                if g != BASE and g >= N_VECTOR:
+                    emit_mult(s, g)
                 if 1 <= j <= N_VECTOR:
-                    emit_mult(k - 1)
+                    emit_mult(s, j - 1)
                 if j == 6 and quantise_next is not None:
                     quantise_next(0, SPAN)
-        for a in range(NU - LAG, NU):
-            emit_acc(a)
-        emit_out(NSPAN - 1)
+        for step in range(NJ, OUT_STEP + 1):
+            emit_sums(NSPAN - 1, step)

@@ -25,13 +25,14 @@ NB = 2 * NU
 FLOPS = 2 * B * O * (I + I * G)
 BASE = 8
 STEPS = [0, 1, 2, BASE, 3, 4, 5, 6, 7]
-SUMS = {6: [0], 7: [1], 8: [2, 3], 9: [4], 10: [5], 11: [6], 13: [7]}
-OUT_STEP = 14
+SUM_AT = 6
 S_AHEAD = 4
 E_BUFS = 8
-R_BUFS = 9
-N_VECTOR = 2
+R_BUFS = 10
+ON_VECTOR = (0, 1)
+ON_VECTOR_LAST = (0, 1, 3)
 X_TASK = 3
+QUANT_AT = 7
 
 
 def tile_rbfkanlayer_t_kernel(tc, x, spline_weight, base_weight, grid, grad_out, out):
@@ -51,10 +52,11 @@ def tile_rbfkanlayer_t_kernel(tc, x, spline_weight, base_weight, grid, grad_out,
         epool = ctx.enter_context(tc.tile_pool(name="epool", bufs=E_BUFS))
         rpool = ctx.enter_context(tc.tile_pool(name="rpool", bufs=R_BUFS))
         opool = ctx.enter_context(tc.tile_pool(name="opool", bufs=2))
-        tp = ctx.enter_context(tc.psum_pool(name="tp", bufs=2))
+        tp = ctx.enter_context(tc.psum_pool(name="tp", bufs=1))
         xp = ctx.enter_context(tc.psum_pool(name="xp", bufs=1))
-        qp = ctx.enter_context(tc.psum_pool(name="qp", bufs=3))
+        qp = ctx.enter_context(tc.psum_pool(name="qp", bufs=4))
         accp = ctx.enter_context(tc.psum_pool(name="accp", bufs=2))
+        ctx.enter_context(tc.manual_schedule())
 
         grid_bf = const.tile([P, G], BF16, name="grid_bf")
         nc.sync.dma_start(out=grid_bf[:], in_=grid.partition_broadcast(P))
@@ -79,9 +81,9 @@ def tile_rbfkanlayer_t_kernel(tc, x, spline_weight, base_weight, grid, grad_out,
         g_sb.append(g_t)
         nc.sync.dma_start(out=g_t[:, 0:4, :], in_=gv[:, 0:4, :])
         nc.sync.dma_start(out=g_t[:, 4:8, :], in_=gv[:, 4:8, :])
-        load_x(1)
         w_b = const.tile([P, G - 2, O], BF16, name="w_b")
         nc.sync.dma_start(out=w_b[:], in_=wv[:, 2:G, :])
+        load_x(1)
         for s in range(1, NSPAN):
             g_t = gpool.tile([P, SPAN_T, O], BF16, name="g_sb", tag="g_sb")
             nc.sync.dma_start(out=g_t[:], in_=gv[:, s * SPAN_T : (s + 1) * SPAN_T, :])
@@ -96,17 +98,17 @@ def tile_rbfkanlayer_t_kernel(tc, x, spline_weight, base_weight, grid, grad_out,
         make_identity(nc, ident_b[:])
         ident_f = const.tile([P, P], F32, name="ident_f")
         make_identity(nc, ident_f[:])
-        c_pos = const.tile([P, G], F32, name="c_pos")
-        nc.vector.tensor_copy(out=c_pos[:], in_=grid_bf[:])
         c_neg = const.tile([P, G], F32, name="c_neg")
         nc.vector.tensor_scalar_mul(out=c_neg[:], in0=grid_bf[:], scalar1=-1.0)
+        c_pos = const.tile([P, G], F32, name="c_pos")
+        nc.vector.tensor_copy(out=c_pos[:], in_=grid_bf[:])
 
         xT = {}
         xT_ps = {}
         g_codes = {}
 
-        def words_pe(src0, src1):
-            ps = tp.tile([P, 2, 2 * P], F32, name="ps_w", tag="tp")
+        def words_pe(src0, src1, pool=tp, tag="tp"):
+            ps = pool.tile([P, 2, 2 * P], F32, name="ps_w", tag=tag)
             for j, src in enumerate((src0, src1)):
                 for u in range(2):
                     nc.tensor.transpose(
@@ -116,24 +118,20 @@ def tile_rbfkanlayer_t_kernel(tc, x, spline_weight, base_weight, grid, grad_out,
                     )
             return ps
 
-        def x_transposed(s, pool, tag):
-            ps = pool.tile([P, SPAN], BF16, name="ps_x", tag=tag)
-            for tt in range(SPAN_T):
-                nc.tensor.transpose(out=ps[:, tt * P : (tt + 1) * P], in_=x_sb[s][:, tt, :], identity=ident_b[:])
-            return ps
-
         def words_copy(ps, dst):
             nc.vector.tensor_copy(out=dst, in_=ps[:].rearrange("p u n -> p n u"))
 
         def prep_tasks(s):
             def x_pe():
-                return x_transposed(s, xp, "xp")
+                ps = xp.tile([P, SPAN], BF16, name="ps_x", tag="xp")
+                for tt in range(SPAN_T):
+                    nc.tensor.transpose(out=ps[:, tt * P : (tt + 1) * P], in_=x_sb[s][:, tt, :], identity=ident_b[:])
+                return ps
 
             def x_copy(ps):
-                if s not in xT:
-                    xt = xtpool.tile([P, SPAN], BF16, name="xT", tag="xT")
-                    nc.vector.tensor_copy(out=xt[:], in_=ps[:])
-                    xT[s] = xt
+                xt = xtpool.tile([P, SPAN], BF16, name="xT", tag="xT")
+                nc.vector.tensor_copy(out=xt[:], in_=ps[:])
+                xT[s] = xt
                 xT_ps[s] = ps
 
             gq = gqpool.tile([P, 4 * SPAN], BF16, name="gq", tag="gq", align_bytes=64)
@@ -145,17 +143,15 @@ def tile_rbfkanlayer_t_kernel(tc, x, spline_weight, base_weight, grid, grad_out,
             for b in range(4):
                 tasks.append(
                     (
-                        lambda b=b: words_pe(g_sb[s][:, 2 * b, :], g_sb[s][:, 2 * b + 1, :]),
+                        lambda pool=tp, tag="tp", b=b: words_pe(g_sb[s][:, 2 * b, :], g_sb[s][:, 2 * b + 1, :], pool, tag),
                         lambda ps, b=b: words_copy(ps, gq_f[:, 2 * P * b : 2 * P * (b + 1), :]),
                     )
                 )
 
-            tasks.insert(X_TASK, (x_pe, x_copy))
-
             def quantise(c0, c1):
                 nc.vector.quantize_mx(out=gc[:, c0:c1].bitcast(E5X4), scales=gs[:, c0:c1], in_=gq[:, 4 * c0 : 4 * c1])
 
-            return tasks, quantise
+            return tasks, (x_pe, x_copy), quantise
 
         wq = const.tile([P, 4 * NJ * I], BF16, name="wq", align_bytes=64)
         wc = const.tile([P, NJ * I], U32, name="wc", align_bytes=64)
@@ -165,36 +161,43 @@ def tile_rbfkanlayer_t_kernel(tc, x, spline_weight, base_weight, grid, grad_out,
         def w_quant(c0, c1):
             nc.vector.quantize_mx(out=wc[:, c0:c1].bitcast(E4X4), scales=ws[:, c0:c1], in_=wq[:, 4 * c0 : 4 * c1])
 
-        def w_pairs(pairs):
-            for b in pairs:
-                ps = words_pe(w_rows(2 * b), w_rows(2 * b + 1))
-                words_copy(ps, wq_f[:, 2 * P * b : 2 * P * (b + 1), :])
-            w_quant(2 * I * pairs[0], 2 * I * (pairs[-1] + 1))
+        def w_pe(b, pool, tag):
+            return words_pe(w_rows(2 * b), w_rows(2 * b + 1), pool, tag)
 
-        def w_base():
+        def w_copy(b, ps):
+            words_copy(ps, wq_f[:, 2 * P * b : 2 * P * (b + 1), :])
+
+        def w_pair_quant(b):
+            w_quant(2 * I * b, 2 * I * (b + 1))
+
+        def w_base_copy():
             nc.vector.tensor_copy(
                 out=wq[:, 4 * G * I : 4 * NJ * I].rearrange("p (c t) -> p c t", t=4),
                 in_=wb_raw[:].rearrange("p t c -> p c t"),
             )
+
+        def w_base_quant():
             w_quant(G * I, NJ * I)
 
-        first, first_quantise = prep_tasks(0)
-        x_pe, x_copy = first.pop(X_TASK)
+        g_words, (x_pe, x_copy), quantise = prep_tasks(0)
         x_copy(x_pe())
-        w_pairs([0])
-        for b in range(4):
-            pe_part, v_part = first[b]
-            v_part(pe_part())
-            if b % 2 == 1:
-                first_quantise(b // 2 * HALF, (b // 2 + 1) * HALF)
-
-        def x_second():
-            ps = x_transposed(1, tp, "tp")
-            xt = xtpool.tile([P, SPAN], BF16, name="xT", tag="xT")
-            nc.vector.tensor_copy(out=xt[:], in_=ps[:])
-            xT[1] = xt
-
-        head_rest = [lambda: w_pairs([1]), w_base, x_second, lambda: w_pairs([2, 3])]
+        ps_w0 = w_pe(0, qp, "q")
+        ps_g0 = g_words[0][0](qp, "q")
+        ps_g1 = g_words[1][0](qp, "q")
+        w_copy(0, ps_w0)
+        g_words[0][1](ps_g0)
+        w_pair_quant(0)
+        g_words[1][1](ps_g1)
+        w_base_copy()
+        ps_w1 = w_pe(1, qp, "q")
+        ps_g2 = g_words[2][0](qp, "q")
+        ps_g3 = g_words[3][0](qp, "q")
+        quantise(0, HALF)
+        g_words[2][1](ps_g2)
+        g_words[3][1](ps_g3)
+        w_copy(1, ps_w1)
+        quantise(HALF, SPAN)
+        w_base_quant()
 
         e_of = {}
         q_of = {}
@@ -202,6 +205,9 @@ def tile_rbfkanlayer_t_kernel(tc, x, spline_weight, base_weight, grid, grad_out,
 
         def unit(k):
             return k // NJ, STEPS[k % NJ]
+
+        def on_vector(s, g):
+            return g in (ON_VECTOR_LAST if s == NSPAN - 1 else ON_VECTOR)
 
         def emit_scalar(k):
             if k >= NU:
@@ -251,7 +257,7 @@ def tile_rbfkanlayer_t_kernel(tc, x, spline_weight, base_weight, grid, grad_out,
             s, g = unit(n // 2)
             part = slice(n % 2 * HALF, (n % 2 + 1) * HALF)
             if g == BASE:
-                r = r_of[s, N_VECTOR - 1]
+                r = r_of[s, ON_VECTOR[-1]]
                 nc.vector.scalar_tensor_tensor(
                     out=r[:, part], in0=q_of[n][:], scalar=-1.0 / 40.0, in1=r[:, part], op0=ALU.mult, op1=ALU.add
                 )
@@ -259,7 +265,7 @@ def tile_rbfkanlayer_t_kernel(tc, x, spline_weight, base_weight, grid, grad_out,
             if n % 2 == 0:
                 r_of[s, g] = rpool.tile([P, SPAN], F32, name="r", tag="r")
             r = r_of[s, g]
-            if g < N_VECTOR:
+            if on_vector(s, g):
                 nc.vector.tensor_tensor(out=r[:, part], in0=q_of[n][:], in1=e_of[s, g][:, part], op=ALU.mult)
             else:
                 nc.vector.scalar_tensor_tensor(
@@ -273,7 +279,7 @@ def tile_rbfkanlayer_t_kernel(tc, x, spline_weight, base_weight, grid, grad_out,
 
         def emit_mult(s, g):
             r = r_of[s, g]
-            if g < N_VECTOR:
+            if on_vector(s, g):
                 nc.vector.scalar_tensor_tensor(
                     out=r[:], in0=xT_ps[s][:], scalar=c_pos[:, g : g + 1], in1=r[:], op0=ALU.subtract, op1=ALU.mult
                 )
@@ -289,7 +295,7 @@ def tile_rbfkanlayer_t_kernel(tc, x, spline_weight, base_weight, grid, grad_out,
             last_span = s == NSPAN - 1
             for h in range(2):
                 dst = o_sb[:, 4 * h : 4 * h + 4, :].rearrange("p t i -> p (t i)")
-                if h == 0:
+                if last_span and h == 0:
                     nc.scalar.activation(out=dst, in_=acc_of[s][h][:], func=ACT.Copy, scale=-40.0)
                 else:
                     nc.vector.tensor_scalar_mul(out=dst, in0=acc_of[s][h][:], scalar1=-40.0)
@@ -299,54 +305,51 @@ def tile_rbfkanlayer_t_kernel(tc, x, spline_weight, base_weight, grid, grad_out,
             if not last_span:
                 nc.sync.dma_start(out=ov[:, s * SPAN_T : (s + 1) * SPAN_T, :], in_=o_sb[:])
 
-        def emit_sums(s, step):
-            if s >= 0:
-                for g in SUMS.get(step, []):
-                    emit_sum(s, g)
-                if step == OUT_STEP:
-                    emit_out(s)
-
         for k in range(S_AHEAD):
             emit_scalar(k)
         emit_mx(0)
         emit_mx(1)
-        tasks = []
-        quantise_next = None
-        task_i = 0
-        head_i = 0
-        pending = None
-        for n in range(NB):
-            k, h = n // 2, n % 2
+        w_pair_quant(1)
+
+        quantise = None
+        copy_due = None
+        for k in range(NU):
             s, j = k // NJ, k % NJ
             g = STEPS[j]
-            if h == 0:
-                emit_scalar(k + S_AHEAD)
-                if j == 0:
-                    tasks, quantise_next, task_i = [], None, 0
-                    if s + 1 < NSPAN:
-                        tasks, quantise_next = prep_tasks(s + 1)
-            else:
-                emit_sums(s - 1, NJ + j)
-                emit_sums(s, j)
-            fresh = None
-            if h == 1 and task_i < len(tasks):
-                pe_part, v_part = tasks[task_i]
-                task_i += 1
-                fresh = (v_part, pe_part())
-            emit_mx(n + 2)
-            emit_evac(n)
-            if h == 1:
-                if pending is not None:
-                    pending[0](pending[1])
-                pending = fresh
-                if head_i < len(head_rest):
-                    head_rest[head_i]()
-                    head_i += 1
-                if g != BASE and g >= N_VECTOR:
-                    emit_mult(s, g)
-                if 1 <= j <= N_VECTOR:
-                    emit_mult(s, j - 1)
-                if j == 6 and quantise_next is not None:
-                    quantise_next(0, SPAN)
-        for step in range(NJ, OUT_STEP + 1):
-            emit_sums(NSPAN - 1, step)
+            if j == 0:
+                words, x_task, quantise = prep_tasks(s + 1) if s + 1 < NSPAN else ([], None, None)
+                tasks = {}
+                if s == 0:
+                    for b in (2, 3):
+                        tasks[b - 2] = (lambda b=b: w_pe(b, tp, "tp"), lambda ps, b=b: w_copy(b, ps))
+                free = [t for t in range(NJ) if t not in tasks and t != X_TASK]
+                for t, task in zip(free, words):
+                    tasks[t] = task
+                if x_task is not None:
+                    tasks[X_TASK] = x_task
+            emit_scalar(k + S_AHEAD)
+            emit_mx(2 * k + 2)
+            emit_mx(2 * k + 3)
+            if k >= SUM_AT and (k - SUM_AT) % NJ < G:
+                emit_sum((k - SUM_AT) // NJ, (k - SUM_AT) % NJ)
+            emit_evac(2 * k)
+            if copy_due is not None:
+                copy_due()
+                copy_due = None
+            if j in tasks:
+                pe_part, v_part = tasks[j]
+                copy_due = lambda v_part=v_part, ps=pe_part(): v_part(ps)
+            if j > 0 and STEPS[j - 1] != BASE and on_vector(s, STEPS[j - 1]):
+                emit_mult(s, STEPS[j - 1])
+            if k > SUM_AT and (k - SUM_AT) % NJ == G:
+                emit_out((k - SUM_AT) // NJ)
+            emit_evac(2 * k + 1)
+            if g != BASE and not on_vector(s, g):
+                emit_mult(s, g)
+            if s == 0 and j in (2, 3):
+                w_pair_quant(j)
+            if j == QUANT_AT and quantise is not None:
+                quantise(0, SPAN)
+        for a in range(NJ - SUM_AT, G):
+            emit_sum(NSPAN - 1, a)
+        emit_out(NSPAN - 1)

@@ -31,8 +31,11 @@ E_BUFS = 8
 R_BUFS = 10
 ON_VECTOR = (0, 1)
 ON_VECTOR_LAST = (0, 1, 3)
-X_TASK = 3
-QUANT_AT = 7
+WORDS_AT = (-2, -1, 0, 1)
+X_AT = 3
+QUANT_AT = 2
+FIRST_WORDS_AT = (2, 4, 5, 6)
+FIRST_QUANT_AT = 7
 
 
 def tile_rbfkanlayer_t_kernel(tc, x, spline_weight, base_weight, grid, grad_out, out):
@@ -121,6 +124,13 @@ def tile_rbfkanlayer_t_kernel(tc, x, spline_weight, base_weight, grid, grad_out,
         def words_copy(ps, dst):
             nc.vector.tensor_copy(out=dst, in_=ps[:].rearrange("p u n -> p n u"))
 
+        gq_of = {}
+
+        def grouped(s):
+            if s not in gq_of:
+                gq_of[s] = gqpool.tile([P, 4 * SPAN], BF16, name="gq", tag="gq", align_bytes=64)
+            return gq_of[s][:].bitcast(F32).rearrange("p (n u) -> p n u", u=2)
+
         def prep_tasks(s):
             def x_pe():
                 ps = xp.tile([P, SPAN], BF16, name="ps_x", tag="xp")
@@ -134,22 +144,22 @@ def tile_rbfkanlayer_t_kernel(tc, x, spline_weight, base_weight, grid, grad_out,
                 xT[s] = xt
                 xT_ps[s] = ps
 
-            gq = gqpool.tile([P, 4 * SPAN], BF16, name="gq", tag="gq", align_bytes=64)
-            gq_f = gq[:].bitcast(F32).rearrange("p (n u) -> p n u", u=2)
-            gc = gcpool.tile([P, SPAN], U32, name="gc", tag="gc", align_bytes=64)
-            gs = gcpool.tile([P, SPAN], U8, name="gs", tag="gs", align_bytes=64)
-            g_codes[s] = (gc, gs)
             tasks = []
             for b in range(4):
                 tasks.append(
                     (
                         lambda pool=tp, tag="tp", b=b: words_pe(g_sb[s][:, 2 * b, :], g_sb[s][:, 2 * b + 1, :], pool, tag),
-                        lambda ps, b=b: words_copy(ps, gq_f[:, 2 * P * b : 2 * P * (b + 1), :]),
+                        lambda ps, b=b: words_copy(ps, grouped(s)[:, 2 * P * b : 2 * P * (b + 1), :]),
                     )
                 )
 
             def quantise(c0, c1):
-                nc.vector.quantize_mx(out=gc[:, c0:c1].bitcast(E5X4), scales=gs[:, c0:c1], in_=gq[:, 4 * c0 : 4 * c1])
+                if s not in g_codes:
+                    gc = gcpool.tile([P, SPAN], U32, name="gc", tag="gc", align_bytes=64)
+                    gs = gcpool.tile([P, SPAN], U8, name="gs", tag="gs", align_bytes=64)
+                    g_codes[s] = (gc, gs)
+                gc, gs = g_codes[s]
+                nc.vector.quantize_mx(out=gc[:, c0:c1].bitcast(E5X4), scales=gs[:, c0:c1], in_=gq_of[s][:, 4 * c0 : 4 * c1])
 
             return tasks, (x_pe, x_copy), quantise
 
@@ -266,7 +276,7 @@ def tile_rbfkanlayer_t_kernel(tc, x, spline_weight, base_weight, grid, grad_out,
                 r_of[s, g] = rpool.tile([P, SPAN], F32, name="r", tag="r")
             r = r_of[s, g]
             if on_vector(s, g):
-                nc.vector.tensor_tensor(out=r[:, part], in0=q_of[n][:], in1=e_of[s, g][:, part], op=ALU.mult)
+                nc.vector.tensor_tensor(out=r[:, part], in0=e_of[s, g][:, part], in1=q_of[n][:], op=ALU.mult)
             else:
                 nc.vector.scalar_tensor_tensor(
                     out=r[:, part],
@@ -311,22 +321,19 @@ def tile_rbfkanlayer_t_kernel(tc, x, spline_weight, base_weight, grid, grad_out,
         emit_mx(1)
         w_pair_quant(1)
 
-        quantise = None
+        transposed = {b - 2: (lambda b=b: w_pe(b, tp, "tp"), lambda ps, b=b: w_copy(b, ps)) for b in (2, 3)}
+        quantise_at = {}
+        for s in range(1, NSPAN):
+            start = (s - 1) * NJ
+            words, x_task, quantise = prep_tasks(s)
+            for b, task in enumerate(words):
+                transposed[FIRST_WORDS_AT[b] if s == 1 else start + WORDS_AT[b]] = task
+            transposed[start + X_AT] = x_task
+            quantise_at[FIRST_QUANT_AT if s == 1 else start + QUANT_AT] = quantise
         copy_due = None
         for k in range(NU):
             s, j = k // NJ, k % NJ
             g = STEPS[j]
-            if j == 0:
-                words, x_task, quantise = prep_tasks(s + 1) if s + 1 < NSPAN else ([], None, None)
-                tasks = {}
-                if s == 0:
-                    for b in (2, 3):
-                        tasks[b - 2] = (lambda b=b: w_pe(b, tp, "tp"), lambda ps, b=b: w_copy(b, ps))
-                free = [t for t in range(NJ) if t not in tasks and t != X_TASK]
-                for t, task in zip(free, words):
-                    tasks[t] = task
-                if x_task is not None:
-                    tasks[X_TASK] = x_task
             emit_scalar(k + S_AHEAD)
             emit_mx(2 * k + 2)
             emit_mx(2 * k + 3)
@@ -336,20 +343,20 @@ def tile_rbfkanlayer_t_kernel(tc, x, spline_weight, base_weight, grid, grad_out,
             if copy_due is not None:
                 copy_due()
                 copy_due = None
-            if j in tasks:
-                pe_part, v_part = tasks[j]
+            if k in transposed:
+                pe_part, v_part = transposed[k]
                 copy_due = lambda v_part=v_part, ps=pe_part(): v_part(ps)
             if j > 0 and STEPS[j - 1] != BASE and on_vector(s, STEPS[j - 1]):
                 emit_mult(s, STEPS[j - 1])
+            if k in quantise_at:
+                quantise_at[k](0, SPAN)
             if k > SUM_AT and (k - SUM_AT) % NJ == G:
                 emit_out((k - SUM_AT) // NJ)
             emit_evac(2 * k + 1)
             if g != BASE and not on_vector(s, g):
                 emit_mult(s, g)
-            if s == 0 and j in (2, 3):
-                w_pair_quant(j)
-            if j == QUANT_AT and quantise is not None:
-                quantise(0, SPAN)
-        for a in range(NJ - SUM_AT, G):
-            emit_sum(NSPAN - 1, a)
+            if k in (2, 3):
+                w_pair_quant(k)
+        for g in range(NJ - SUM_AT, G):
+            emit_sum(NSPAN - 1, g)
         emit_out(NSPAN - 1)

@@ -26,10 +26,10 @@ FLOPS = 2 * B * O * (I + I * G)
 BASE = 8
 STEPS = [0, 1, 2, BASE, 3, 4, 5, 6, 7]
 SUM_AT = 6
-S_AHEAD = 4
+S_AHEAD = 3
 E_BUFS = 8
 R_BUFS = 10
-ON_VECTOR = (0, 1)
+ON_VECTOR = (0,)
 ON_VECTOR_LAST = (0, 1, 3)
 WORDS_AT = (-2, -1, 0, 1)
 X_AT = 3
@@ -228,7 +228,11 @@ def tile_rbfkanlayer_t_kernel(tc, x, spline_weight, base_weight, grid, grad_out,
             e = epool.tile([P, SPAN], F32, name="e", tag="e")
             e_of[s, g] = e
             nc.scalar.activation(out=e[:], in_=xT[s][:], func=ACT.Square, bias=c_neg[:, g : g + 1], scale=1.0)
-            nc.scalar.activation(out=e[:], in_=e[:], func=ACT.Exp, scale=-20.0)
+
+        def emit_exp(k):
+            if k < NU and unit(k)[1] != BASE:
+                e = e_of[unit(k)]
+                nc.scalar.activation(out=e[:], in_=e[:], func=ACT.Exp, scale=-20.0)
 
         def emit_mx(n):
             if n >= NB:
@@ -237,6 +241,8 @@ def tile_rbfkanlayer_t_kernel(tc, x, spline_weight, base_weight, grid, grad_out,
             s, g = unit(n // 2)
             gc, gs = g_codes[s]
             q = qp.tile([P, HALF], F32, name="q", tag="q")
+            if h == 0:
+                nc.tensor.matmul(out=q[:, 0:256], lhsT=ident_b[:], rhs=xT[s][:, 0:256], start=True, stop=True)
             nc.tensor.matmul_mx(
                 out=q[:],
                 lhsT=wc[:, g * I : (g + 1) * I].bitcast(E4X4),
@@ -305,7 +311,7 @@ def tile_rbfkanlayer_t_kernel(tc, x, spline_weight, base_weight, grid, grad_out,
             last_span = s == NSPAN - 1
             for h in range(2):
                 dst = o_sb[:, 4 * h : 4 * h + 4, :].rearrange("p t i -> p (t i)")
-                if last_span and h == 0:
+                if h == 0:
                     nc.scalar.activation(out=dst, in_=acc_of[s][h][:], func=ACT.Copy, scale=-40.0)
                 else:
                     nc.vector.tensor_scalar_mul(out=dst, in0=acc_of[s][h][:], scalar1=-40.0)
@@ -317,6 +323,8 @@ def tile_rbfkanlayer_t_kernel(tc, x, spline_weight, base_weight, grid, grad_out,
 
         for k in range(S_AHEAD):
             emit_scalar(k)
+            if k > 0:
+                emit_exp(k - 1)
         emit_mx(0)
         emit_mx(1)
         w_pair_quant(1)
@@ -335,6 +343,7 @@ def tile_rbfkanlayer_t_kernel(tc, x, spline_weight, base_weight, grid, grad_out,
             s, j = k // NJ, k % NJ
             g = STEPS[j]
             emit_scalar(k + S_AHEAD)
+            emit_exp(k + S_AHEAD - 1)
             emit_mx(2 * k + 2)
             emit_mx(2 * k + 3)
             if k >= SUM_AT and (k - SUM_AT) % NJ < G:

@@ -29,7 +29,8 @@ SUM_AT = 6
 S_AHEAD = 3
 E_BUFS = 8
 R_BUFS = 10
-ON_VECTOR = (0,)
+ON_VECTOR = (0, 1)
+ON_VECTOR_ODD = (0,)
 ON_VECTOR_LAST = (0, 1, 3)
 WORDS_AT = (-2, -1, 0, 1)
 X_AT = 3
@@ -217,7 +218,7 @@ def tile_rbfkanlayer_t_kernel(tc, x, spline_weight, base_weight, grid, grad_out,
             return k // NJ, STEPS[k % NJ]
 
         def on_vector(s, g):
-            return g in (ON_VECTOR_LAST if s == NSPAN - 1 else ON_VECTOR)
+            return g in (ON_VECTOR_LAST if s == NSPAN - 1 else ON_VECTOR_ODD if s % 2 else ON_VECTOR)
 
         def emit_scalar(k):
             if k >= NU:
@@ -241,8 +242,6 @@ def tile_rbfkanlayer_t_kernel(tc, x, spline_weight, base_weight, grid, grad_out,
             s, g = unit(n // 2)
             gc, gs = g_codes[s]
             q = qp.tile([P, HALF], F32, name="q", tag="q")
-            if h == 0:
-                nc.tensor.matmul(out=q[:, 0:256], lhsT=ident_b[:], rhs=xT[s][:, 0:256], start=True, stop=True)
             nc.tensor.matmul_mx(
                 out=q[:],
                 lhsT=wc[:, g * I : (g + 1) * I].bitcast(E4X4),
@@ -273,7 +272,7 @@ def tile_rbfkanlayer_t_kernel(tc, x, spline_weight, base_weight, grid, grad_out,
             s, g = unit(n // 2)
             part = slice(n % 2 * HALF, (n % 2 + 1) * HALF)
             if g == BASE:
-                r = r_of[s, ON_VECTOR[-1]]
+                r = r_of[s, 0]
                 nc.vector.scalar_tensor_tensor(
                     out=r[:, part], in0=q_of[n][:], scalar=-1.0 / 40.0, in1=r[:, part], op0=ALU.mult, op1=ALU.add
                 )
@@ -311,7 +310,7 @@ def tile_rbfkanlayer_t_kernel(tc, x, spline_weight, base_weight, grid, grad_out,
             last_span = s == NSPAN - 1
             for h in range(2):
                 dst = o_sb[:, 4 * h : 4 * h + 4, :].rearrange("p t i -> p (t i)")
-                if h == 0:
+                if last_span and h == 0:
                     nc.scalar.activation(out=dst, in_=acc_of[s][h][:], func=ACT.Copy, scale=-40.0)
                 else:
                     nc.vector.tensor_scalar_mul(out=dst, in0=acc_of[s][h][:], scalar1=-40.0)
@@ -346,22 +345,22 @@ def tile_rbfkanlayer_t_kernel(tc, x, spline_weight, base_weight, grid, grad_out,
             emit_exp(k + S_AHEAD - 1)
             emit_mx(2 * k + 2)
             emit_mx(2 * k + 3)
-            if k >= SUM_AT and (k - SUM_AT) % NJ < G:
-                emit_sum((k - SUM_AT) // NJ, (k - SUM_AT) % NJ)
             emit_evac(2 * k)
+            emit_evac(2 * k + 1)
             if copy_due is not None:
                 copy_due()
                 copy_due = None
             if k in transposed:
                 pe_part, v_part = transposed[k]
                 copy_due = lambda v_part=v_part, ps=pe_part(): v_part(ps)
+            if k >= SUM_AT and (k - SUM_AT) % NJ < G:
+                emit_sum((k - SUM_AT) // NJ, (k - SUM_AT) % NJ)
             if j > 0 and STEPS[j - 1] != BASE and on_vector(s, STEPS[j - 1]):
                 emit_mult(s, STEPS[j - 1])
             if k in quantise_at:
                 quantise_at[k](0, SPAN)
             if k > SUM_AT and (k - SUM_AT) % NJ == G:
                 emit_out((k - SUM_AT) // NJ)
-            emit_evac(2 * k + 1)
             if g != BASE and not on_vector(s, g):
                 emit_mult(s, g)
             if k in (2, 3):

@@ -30,8 +30,8 @@ S_AHEAD = 3
 E_BUFS = 8
 R_BUFS = 10
 ON_VECTOR = (0, 1)
-ON_VECTOR_ODD = (0,)
 ON_VECTOR_LAST = (0, 1, 3)
+VECTOR_ENDS = (6, 7)
 WORDS_AT = (-2, -1, 0, 1)
 X_AT = 3
 QUANT_AT = 2
@@ -218,7 +218,7 @@ def tile_rbfkanlayer_t_kernel(tc, x, spline_weight, base_weight, grid, grad_out,
             return k // NJ, STEPS[k % NJ]
 
         def on_vector(s, g):
-            return g in (ON_VECTOR_LAST if s == NSPAN - 1 else ON_VECTOR_ODD if s % 2 else ON_VECTOR)
+            return g in (ON_VECTOR_LAST if s == NSPAN - 1 else ON_VECTOR)
 
         def emit_scalar(k):
             if k >= NU:
@@ -272,7 +272,7 @@ def tile_rbfkanlayer_t_kernel(tc, x, spline_weight, base_weight, grid, grad_out,
             s, g = unit(n // 2)
             part = slice(n % 2 * HALF, (n % 2 + 1) * HALF)
             if g == BASE:
-                r = r_of[s, 0]
+                r = r_of[s, ON_VECTOR[-1]]
                 nc.vector.scalar_tensor_tensor(
                     out=r[:, part], in0=q_of[n][:], scalar=-1.0 / 40.0, in1=r[:, part], op0=ALU.mult, op1=ALU.add
                 )
@@ -298,7 +298,7 @@ def tile_rbfkanlayer_t_kernel(tc, x, spline_weight, base_weight, grid, grad_out,
                 nc.vector.scalar_tensor_tensor(
                     out=r[:], in0=xT_ps[s][:], scalar=c_pos[:, g : g + 1], in1=r[:], op0=ALU.subtract, op1=ALU.mult
                 )
-            elif s == NSPAN - 1 and g == G - 1:
+            elif s == NSPAN - 1 and g in VECTOR_ENDS:
                 for h in range(2):
                     part = slice(h * HALF, (h + 1) * HALF)
                     nc.vector.tensor_tensor(out=r[:, part], in0=r[:, part], in1=e_of[s, g][:, part], op=ALU.mult)
@@ -310,7 +310,7 @@ def tile_rbfkanlayer_t_kernel(tc, x, spline_weight, base_weight, grid, grad_out,
             last_span = s == NSPAN - 1
             for h in range(2):
                 dst = o_sb[:, 4 * h : 4 * h + 4, :].rearrange("p t i -> p (t i)")
-                if last_span and h == 0:
+                if h == 0:
                     nc.scalar.activation(out=dst, in_=acc_of[s][h][:], func=ACT.Copy, scale=-40.0)
                 else:
                     nc.vector.tensor_scalar_mul(out=dst, in0=acc_of[s][h][:], scalar1=-40.0)
@@ -346,7 +346,8 @@ def tile_rbfkanlayer_t_kernel(tc, x, spline_weight, base_weight, grid, grad_out,
             emit_mx(2 * k + 2)
             emit_mx(2 * k + 3)
             emit_evac(2 * k)
-            emit_evac(2 * k + 1)
+            if j > 0 and STEPS[j - 1] != BASE and on_vector(s, STEPS[j - 1]):
+                emit_mult(s, STEPS[j - 1])
             if copy_due is not None:
                 copy_due()
                 copy_due = None
@@ -355,8 +356,7 @@ def tile_rbfkanlayer_t_kernel(tc, x, spline_weight, base_weight, grid, grad_out,
                 copy_due = lambda v_part=v_part, ps=pe_part(): v_part(ps)
             if k >= SUM_AT and (k - SUM_AT) % NJ < G:
                 emit_sum((k - SUM_AT) // NJ, (k - SUM_AT) % NJ)
-            if j > 0 and STEPS[j - 1] != BASE and on_vector(s, STEPS[j - 1]):
-                emit_mult(s, STEPS[j - 1])
+            emit_evac(2 * k + 1)
             if k in quantise_at:
                 quantise_at[k](0, SPAN)
             if k > SUM_AT and (k - SUM_AT) % NJ == G:

@@ -30,12 +30,11 @@ S_AHEAD = 3
 E_BUFS = 8
 R_BUFS = 10
 ON_VECTOR = (0, 1)
-ON_VECTOR_LAST = (0, 1, 3)
-VECTOR_ENDS = (6, 7)
+ON_VECTOR_LAST = (0, 1, 3, 6, 7)
 WORDS_AT = (-2, -1, 0, 1)
-X_AT = 3
+X_AT = 2
 QUANT_AT = 2
-FIRST_WORDS_AT = (2, 4, 5, 6)
+FIRST_WORDS_AT = (3, 4, 5, 6)
 FIRST_QUANT_AT = 7
 
 
@@ -62,8 +61,10 @@ def tile_rbfkanlayer_t_kernel(tc, x, spline_weight, base_weight, grid, grad_out,
         accp = ctx.enter_context(tc.psum_pool(name="accp", bufs=2))
         ctx.enter_context(tc.manual_schedule())
 
-        grid_bf = const.tile([P, G], BF16, name="grid_bf")
-        nc.sync.dma_start(out=grid_bf[:], in_=grid.partition_broadcast(P))
+        ones = const.tile([P, P], BF16, name="ones")
+        nc.vector.memset(ones[:], 1.0)
+        grid_row = const.tile([P, G], BF16, name="grid_row")
+        nc.vector.memset(grid_row[:], 0.0)
         x_sb = []
         g_sb = []
 
@@ -73,6 +74,7 @@ def tile_rbfkanlayer_t_kernel(tc, x, spline_weight, base_weight, grid, grad_out,
             x_sb.append(x_t)
 
         load_x(0)
+        nc.sync.dma_start(out=grid_row[0:1, :], in_=grid.rearrange("(o g) -> o g", o=1))
         w_a = const.tile([P, 2, O], BF16, name="w_a")
         nc.sync.dma_start(out=w_a[:], in_=wv[:, 0:2, :])
         wb_raw = const.tile([P, 4, I], BF16, name="wb_raw")
@@ -103,9 +105,7 @@ def tile_rbfkanlayer_t_kernel(tc, x, spline_weight, base_weight, grid, grad_out,
         ident_f = const.tile([P, P], F32, name="ident_f")
         make_identity(nc, ident_f[:])
         c_neg = const.tile([P, G], F32, name="c_neg")
-        nc.vector.tensor_scalar_mul(out=c_neg[:], in0=grid_bf[:], scalar1=-1.0)
         c_pos = const.tile([P, G], F32, name="c_pos")
-        nc.vector.tensor_copy(out=c_pos[:], in_=grid_bf[:])
 
         xT = {}
         xT_ps = {}
@@ -191,7 +191,12 @@ def tile_rbfkanlayer_t_kernel(tc, x, spline_weight, base_weight, grid, grad_out,
             w_quant(G * I, NJ * I)
 
         g_words, (x_pe, x_copy), quantise = prep_tasks(0)
-        x_copy(x_pe())
+        ps_x = x_pe()
+        ps_c = tp.tile([P, G], F32, name="ps_c", tag="tp")
+        nc.tensor.matmul(out=ps_c[:], lhsT=ones[:], rhs=grid_row[:], start=True, stop=True)
+        x_copy(ps_x)
+        nc.vector.tensor_scalar_mul(out=c_neg[:], in0=ps_c[:], scalar1=-1.0)
+        nc.vector.tensor_copy(out=c_pos[:], in_=ps_c[:])
         ps_w0 = w_pe(0, qp, "q")
         ps_g0 = g_words[0][0](qp, "q")
         ps_g1 = g_words[1][0](qp, "q")
@@ -295,13 +300,17 @@ def tile_rbfkanlayer_t_kernel(tc, x, spline_weight, base_weight, grid, grad_out,
         def emit_mult(s, g):
             r = r_of[s, g]
             if on_vector(s, g):
-                nc.vector.scalar_tensor_tensor(
-                    out=r[:], in0=xT_ps[s][:], scalar=c_pos[:, g : g + 1], in1=r[:], op0=ALU.subtract, op1=ALU.mult
-                )
-            elif s == NSPAN - 1 and g in VECTOR_ENDS:
-                for h in range(2):
-                    part = slice(h * HALF, (h + 1) * HALF)
-                    nc.vector.tensor_tensor(out=r[:, part], in0=r[:, part], in1=e_of[s, g][:, part], op=ALU.mult)
+                width = HALF if (s, g) == (NSPAN - 1, G - 1) else SPAN
+                for c0 in range(0, SPAN, width):
+                    part = slice(c0, c0 + width)
+                    nc.vector.scalar_tensor_tensor(
+                        out=r[:, part],
+                        in0=xT_ps[s][:, part],
+                        scalar=c_pos[:, g : g + 1],
+                        in1=r[:, part],
+                        op0=ALU.subtract,
+                        op1=ALU.mult,
+                    )
             else:
                 nc.gpsimd.tensor_tensor(out=r[:], in0=r[:], in1=e_of[s, g][:], op=ALU.mult)
 
@@ -310,7 +319,7 @@ def tile_rbfkanlayer_t_kernel(tc, x, spline_weight, base_weight, grid, grad_out,
             last_span = s == NSPAN - 1
             for h in range(2):
                 dst = o_sb[:, 4 * h : 4 * h + 4, :].rearrange("p t i -> p (t i)")
-                if h == 0:
+                if s == NSPAN - 2 or (last_span and h == 0):
                     nc.scalar.activation(out=dst, in_=acc_of[s][h][:], func=ACT.Copy, scale=-40.0)
                 else:
                     nc.vector.tensor_scalar_mul(out=dst, in0=acc_of[s][h][:], scalar1=-40.0)
@@ -337,6 +346,13 @@ def tile_rbfkanlayer_t_kernel(tc, x, spline_weight, base_weight, grid, grad_out,
                 transposed[FIRST_WORDS_AT[b] if s == 1 else start + WORDS_AT[b]] = task
             transposed[start + X_AT] = x_task
             quantise_at[FIRST_QUANT_AT if s == 1 else start + QUANT_AT] = quantise
+        sums = {}
+        outs = {}
+        for s in range(NSPAN):
+            for g in range(G):
+                step = s * NJ + SUM_AT + ((g // 2 if g < G - 1 else NJ - SUM_AT) if s == NSPAN - 1 else g)
+                sums.setdefault(step, []).append((s, g))
+            outs[step + 1] = s
         copy_due = None
         for k in range(NU):
             s, j = k // NJ, k % NJ
@@ -354,17 +370,20 @@ def tile_rbfkanlayer_t_kernel(tc, x, spline_weight, base_weight, grid, grad_out,
             if k in transposed:
                 pe_part, v_part = transposed[k]
                 copy_due = lambda v_part=v_part, ps=pe_part(): v_part(ps)
-            if k >= SUM_AT and (k - SUM_AT) % NJ < G:
-                emit_sum((k - SUM_AT) // NJ, (k - SUM_AT) % NJ)
+            for u in sums.get(k, []):
+                emit_sum(*u)
             emit_evac(2 * k + 1)
             if k in quantise_at:
                 quantise_at[k](0, SPAN)
-            if k > SUM_AT and (k - SUM_AT) % NJ == G:
-                emit_out((k - SUM_AT) // NJ)
+            if k in outs:
+                emit_out(outs[k])
             if g != BASE and not on_vector(s, g):
                 emit_mult(s, g)
             if k in (2, 3):
                 w_pair_quant(k)
-        for g in range(NJ - SUM_AT, G):
-            emit_sum(NSPAN - 1, g)
+        for k in range(NU, max(sums) + 1):
+            for s, g in sums[k]:
+                if g == G - 1:
+                    emit_mult(s, g)
+                emit_sum(s, g)
         emit_out(NSPAN - 1)

from contextlib import ExitStack

import concourse.mybir as mybir
from concourse.masks import make_identity

F32 = mybir.dt.float32
BF16 = mybir.dt.bfloat16
U32 = mybir.dt.uint32
U8 = mybir.dt.uint8
E4X4 = mybir.dt.float8_e4m3fn_x4
E5X4 = mybir.dt.float8_e5m2_x4
ACT = mybir.ActivationFunctionType
ALU = mybir.AluOpType

P = 128
B, I, O, G = 8192, 128, 512, 8
NT = B // P
SPAN_T = 8
SPAN = SPAN_T * P
HALF = SPAN // 2
NSPAN = NT // SPAN_T
NJ = G + 1
NU = NSPAN * NJ
NB = 2 * NU
FLOPS = 2 * B * O * (I + I * G)
BASE = 8
STEPS = [0, 1, 2, BASE, 3, 4, 5, 6, 7]
SUM_AT = 6
S_AHEAD = 3
E_BUFS = 8
R_BUFS = 10
ON_VECTOR = (0, 1)
ON_VECTOR_LAST = (0, 1, 3, 6, 7)
WORDS_AT = (-2, -1, 0, 1)
X_AT = 2
QUANT_AT = 2
FIRST_WORDS_AT = (3, 4, 5, 6)
FIRST_QUANT_AT = 7


def tile_rbfkanlayer_t_kernel(tc, x, spline_weight, base_weight, grid, grad_out, out):
    nc = tc.nc
    xv = x.rearrange("(p t) i -> p t i", t=NT)
    gv = grad_out.rearrange("(p t) o -> p t o", t=NT)
    ov = out.rearrange("(p t) i -> p t i", t=NT)
    wv = spline_weight.rearrange("(i g) o -> i g o", g=G)

    with ExitStack() as ctx:
        const = ctx.enter_context(tc.tile_pool(name="const", bufs=1))
        gpool = ctx.enter_context(tc.tile_pool(name="gpool", bufs=NSPAN))
        xpool = ctx.enter_context(tc.tile_pool(name="xpool", bufs=NSPAN))
        xtpool = ctx.enter_context(tc.tile_pool(name="xtpool", bufs=NSPAN))
        gqpool = ctx.enter_context(tc.tile_pool(name="gqpool", bufs=2))
        gcpool = ctx.enter_context(tc.tile_pool(name="gcpool", bufs=2))
        epool = ctx.enter_context(tc.tile_pool(name="epool", bufs=E_BUFS))
        rpool = ctx.enter_context(tc.tile_pool(name="rpool", bufs=R_BUFS))
        opool = ctx.enter_context(tc.tile_pool(name="opool", bufs=2))
        tp = ctx.enter_context(tc.psum_pool(name="tp", bufs=1))
        xp = ctx.enter_context(tc.psum_pool(name="xp", bufs=1))
        qp = ctx.enter_context(tc.psum_pool(name="qp", bufs=4))
        accp = ctx.enter_context(tc.psum_pool(name="accp", bufs=2))
        ctx.enter_context(tc.manual_schedule())

        ones = const.tile([P, P], BF16, name="ones")
        nc.vector.memset(ones[:], 1.0)
        grid_row = const.tile([P, G], BF16, name="grid_row")
        nc.vector.memset(grid_row[:], 0.0)
        x_sb = []
        g_sb = []

        def load_x(s):
            x_t = xpool.tile([P, SPAN_T, I], BF16, name="x_sb", tag="x_sb")
            nc.sync.dma_start(out=x_t[:], in_=xv[:, s * SPAN_T : (s + 1) * SPAN_T, :])
            x_sb.append(x_t)

        load_x(0)
        nc.sync.dma_start(out=grid_row[0:1, :], in_=grid.rearrange("(o g) -> o g", o=1))
        w_a = const.tile([P, 2, O], BF16, name="w_a")
        nc.sync.dma_start(out=w_a[:], in_=wv[:, 0:2, :])
        wb_raw = const.tile([P, 4, I], BF16, name="wb_raw")
        for u in range(2):
            nc.sync.dma_start(
                out=wb_raw[:, 2 * u : 2 * u + 2, :],
                in_=base_weight[256 * u : 256 * u + 256, :].rearrange("(p e) c -> p e c", e=2),
            )
        g_t = gpool.tile([P, SPAN_T, O], BF16, name="g_sb", tag="g_sb")
        g_sb.append(g_t)
        nc.sync.dma_start(out=g_t[:, 0:4, :], in_=gv[:, 0:4, :])
        nc.sync.dma_start(out=g_t[:, 4:8, :], in_=gv[:, 4:8, :])
        w_b = const.tile([P, G - 2, O], BF16, name="w_b")
        nc.sync.dma_start(out=w_b[:], in_=wv[:, 2:G, :])
        load_x(1)
        for s in range(1, NSPAN):
            g_t = gpool.tile([P, SPAN_T, O], BF16, name="g_sb", tag="g_sb")
            nc.sync.dma_start(out=g_t[:], in_=gv[:, s * SPAN_T : (s + 1) * SPAN_T, :])
            g_sb.append(g_t)
            if s + 1 < NSPAN:
                load_x(s + 1)

        def w_rows(g):
            return w_a[:, g, :] if g < 2 else w_b[:, g - 2, :]

        ident_b = const.tile([P, P], BF16, name="ident_b")
        make_identity(nc, ident_b[:])
        ident_f = const.tile([P, P], F32, name="ident_f")
        make_identity(nc, ident_f[:])
        c_neg = const.tile([P, G], F32, name="c_neg")
        c_pos = const.tile([P, G], F32, name="c_pos")

        xT = {}
        xT_ps = {}
        g_codes = {}

        def words_pe(src0, src1, pool=tp, tag="tp"):
            ps = pool.tile([P, 2, 2 * P], F32, name="ps_w", tag=tag)
            for j, src in enumerate((src0, src1)):
                for u in range(2):
                    nc.tensor.transpose(
                        out=ps[:, u, j * P : (j + 1) * P],
                        in_=src.bitcast(F32)[:, u * P : (u + 1) * P],
                        identity=ident_f[:],
                    )
            return ps

        def words_copy(ps, dst):
            nc.vector.tensor_copy(out=dst, in_=ps[:].rearrange("p u n -> p n u"))

        gq_of = {}

        def grouped(s):
            if s not in gq_of:
                gq_of[s] = gqpool.tile([P, 4 * SPAN], BF16, name="gq", tag="gq", align_bytes=64)
            return gq_of[s][:].bitcast(F32).rearrange("p (n u) -> p n u", u=2)

        def prep_tasks(s):
            def x_pe():
                ps = xp.tile([P, SPAN], BF16, name="ps_x", tag="xp")
                for tt in range(SPAN_T):
                    nc.tensor.transpose(out=ps[:, tt * P : (tt + 1) * P], in_=x_sb[s][:, tt, :], identity=ident_b[:])
                return ps

            def x_copy(ps):
                xt = xtpool.tile([P, SPAN], BF16, name="xT", tag="xT")
                nc.vector.tensor_copy(out=xt[:], in_=ps[:])
                xT[s] = xt
                xT_ps[s] = ps

            tasks = []
            for b in range(4):
                tasks.append(
                    (
                        lambda pool=tp, tag="tp", b=b: words_pe(g_sb[s][:, 2 * b, :], g_sb[s][:, 2 * b + 1, :], pool, tag),
                        lambda ps, b=b: words_copy(ps, grouped(s)[:, 2 * P * b : 2 * P * (b + 1), :]),
                    )
                )

            def quantise(c0, c1):
                if s not in g_codes:
                    gc = gcpool.tile([P, SPAN], U32, name="gc", tag="gc", align_bytes=64)
                    gs = gcpool.tile([P, SPAN], U8, name="gs", tag="gs", align_bytes=64)
                    g_codes[s] = (gc, gs)
                gc, gs = g_codes[s]
                nc.vector.quantize_mx(out=gc[:, c0:c1].bitcast(E5X4), scales=gs[:, c0:c1], in_=gq_of[s][:, 4 * c0 : 4 * c1])

            return tasks, (x_pe, x_copy), quantise

        wq = const.tile([P, 4 * NJ * I], BF16, name="wq", align_bytes=64)
        wc = const.tile([P, NJ * I], U32, name="wc", align_bytes=64)
        ws = const.tile([P, NJ * I], U8, name="ws", align_bytes=64)
        wq_f = wq[:, 0 : 4 * G * I].bitcast(F32).rearrange("p (n u) -> p n u", u=2)

        def w_quant(c0, c1):
            nc.vector.quantize_mx(out=wc[:, c0:c1].bitcast(E4X4), scales=ws[:, c0:c1], in_=wq[:, 4 * c0 : 4 * c1])

        def w_pe(b, pool, tag):
            return words_pe(w_rows(2 * b), w_rows(2 * b + 1), pool, tag)

        def w_copy(b, ps):
            words_copy(ps, wq_f[:, 2 * P * b : 2 * P * (b + 1), :])

        def w_pair_quant(b):
            w_quant(2 * I * b, 2 * I * (b + 1))

        def w_base_copy():
            nc.vector.tensor_copy(
                out=wq[:, 4 * G * I : 4 * NJ * I].rearrange("p (c t) -> p c t", t=4),
                in_=wb_raw[:].rearrange("p t c -> p c t"),
            )

        def w_base_quant():
            w_quant(G * I, NJ * I)

        g_words, (x_pe, x_copy), quantise = prep_tasks(0)
        ps_x = x_pe()
        ps_c = tp.tile([P, G], F32, name="ps_c", tag="tp")
        nc.tensor.matmul(out=ps_c[:], lhsT=ones[:], rhs=grid_row[:], start=True, stop=True)
        x_copy(ps_x)
        nc.vector.tensor_scalar_mul(out=c_neg[:], in0=ps_c[:], scalar1=-1.0)
        nc.vector.tensor_copy(out=c_pos[:], in_=ps_c[:])
        ps_w0 = w_pe(0, qp, "q")
        ps_g0 = g_words[0][0](qp, "q")
        ps_g1 = g_words[1][0](qp, "q")
        w_copy(0, ps_w0)
        g_words[0][1](ps_g0)
        w_pair_quant(0)
        g_words[1][1](ps_g1)
        w_base_copy()
        ps_w1 = w_pe(1, qp, "q")
        ps_g2 = g_words[2][0](qp, "q")
        ps_g3 = g_words[3][0](qp, "q")
        quantise(0, HALF)
        g_words[2][1](ps_g2)
        g_words[3][1](ps_g3)
        w_copy(1, ps_w1)
        quantise(HALF, SPAN)
        w_base_quant()

        e_of = {}
        q_of = {}
        r_of = {}

        def unit(k):
            return k // NJ, STEPS[k % NJ]

        def on_vector(s, g):
            return g in (ON_VECTOR_LAST if s == NSPAN - 1 else ON_VECTOR)

        def emit_scalar(k):
            if k >= NU:
                return
            s, g = unit(k)
            if g == BASE:
                return
            e = epool.tile([P, SPAN], F32, name="e", tag="e")
            e_of[s, g] = e
            nc.scalar.activation(out=e[:], in_=xT[s][:], func=ACT.Square, bias=c_neg[:, g : g + 1], scale=1.0)

        def emit_exp(k):
            if k < NU and unit(k)[1] != BASE:
                e = e_of[unit(k)]
                nc.scalar.activation(out=e[:], in_=e[:], func=ACT.Exp, scale=-20.0)

        def emit_mx(n):
            if n >= NB:
                return
            h = n % 2
            s, g = unit(n // 2)
            gc, gs = g_codes[s]
            q = qp.tile([P, HALF], F32, name="q", tag="q")
            nc.tensor.matmul_mx(
                out=q[:],
                lhsT=wc[:, g * I : (g + 1) * I].bitcast(E4X4),
                lhsT_scale=ws[:, g * I : (g + 1) * I],
                rhs=gc[:, h * HALF : (h + 1) * HALF].bitcast(E5X4),
                rhs_scale=gs[:, h * HALF : (h + 1) * HALF],
                start=True,
                stop=True,
            )
            q_of[n] = q

        acc_of = {}

        def emit_sum(s, g):
            if g == 0:
                acc_of[s] = [accp.tile([P, HALF], F32, name="acc%d" % h, tag="acc") for h in range(2)]
            for tt in range(SPAN_T):
                nc.tensor.matmul(
                    out=acc_of[s][tt // 4][:, (tt % 4) * P : (tt % 4 + 1) * P],
                    lhsT=r_of[s, g][:, tt * P : (tt + 1) * P],
                    rhs=ident_f[:],
                    is_transpose=True,
                    start=(g == 0 and tt % 4 == 0),
                    stop=(g == G - 1 and tt % 4 == 3),
                )

        def emit_evac(n):
            s, g = unit(n // 2)
            part = slice(n % 2 * HALF, (n % 2 + 1) * HALF)
            if g == BASE:
                r = r_of[s, ON_VECTOR[-1]]
                nc.vector.scalar_tensor_tensor(
                    out=r[:, part], in0=q_of[n][:], scalar=-1.0 / 40.0, in1=r[:, part], op0=ALU.mult, op1=ALU.add
                )
                return
            if n % 2 == 0:
                r_of[s, g] = rpool.tile([P, SPAN], F32, name="r", tag="r")
            r = r_of[s, g]
            if on_vector(s, g):
                nc.vector.tensor_tensor(out=r[:, part], in0=e_of[s, g][:, part], in1=q_of[n][:], op=ALU.mult)
            else:
                nc.vector.scalar_tensor_tensor(
                    out=r[:, part],
                    in0=xT[s][:, part],
                    scalar=c_pos[:, g : g + 1],
                    in1=q_of[n][:],
                    op0=ALU.subtract,
                    op1=ALU.mult,
                )

        def emit_mult(s, g):
            r = r_of[s, g]
            if on_vector(s, g):
                width = HALF if (s, g) == (NSPAN - 1, G - 1) else SPAN
                for c0 in range(0, SPAN, width):
                    part = slice(c0, c0 + width)
                    nc.vector.scalar_tensor_tensor(
                        out=r[:, part],
                        in0=xT_ps[s][:, part],
                        scalar=c_pos[:, g : g + 1],
                        in1=r[:, part],
                        op0=ALU.subtract,
                        op1=ALU.mult,
                    )
            else:
                nc.gpsimd.tensor_tensor(out=r[:], in0=r[:], in1=e_of[s, g][:], op=ALU.mult)

        def emit_out(s):
            o_sb = opool.tile([P, SPAN_T, I], F32, name="o_sb", tag="o_sb")
            last_span = s == NSPAN - 1
            for h in range(2):
                dst = o_sb[:, 4 * h : 4 * h + 4, :].rearrange("p t i -> p (t i)")
                if s == NSPAN - 2 or (last_span and h == 0):
                    nc.scalar.activation(out=dst, in_=acc_of[s][h][:], func=ACT.Copy, scale=-40.0)
                else:
                    nc.vector.tensor_scalar_mul(out=dst, in0=acc_of[s][h][:], scalar1=-40.0)
                if last_span:
                    t0 = s * SPAN_T + 4 * h
                    nc.sync.dma_start(out=ov[:, t0 : t0 + 4, :], in_=o_sb[:, 4 * h : 4 * h + 4, :])
            if not last_span:
                nc.sync.dma_start(out=ov[:, s * SPAN_T : (s + 1) * SPAN_T, :], in_=o_sb[:])

        for k in range(S_AHEAD):
            emit_scalar(k)
            if k > 0:
                emit_exp(k - 1)
        emit_mx(0)
        emit_mx(1)
        w_pair_quant(1)

        transposed = {b - 2: (lambda b=b: w_pe(b, tp, "tp"), lambda ps, b=b: w_copy(b, ps)) for b in (2, 3)}
        quantise_at = {}
        for s in range(1, NSPAN):
            start = (s - 1) * NJ
            words, x_task, quantise = prep_tasks(s)
            for b, task in enumerate(words):
                transposed[FIRST_WORDS_AT[b] if s == 1 else start + WORDS_AT[b]] = task
            transposed[start + X_AT] = x_task
            quantise_at[FIRST_QUANT_AT if s == 1 else start + QUANT_AT] = quantise
        sums = {}
        outs = {}
        for s in range(NSPAN):
            for g in range(G):
                step = s * NJ + SUM_AT + ((g // 2 if g < G - 1 else NJ - SUM_AT) if s == NSPAN - 1 else g)
                sums.setdefault(step, []).append((s, g))
            outs[step + 1] = s
        copy_due = None
        for k in range(NU):
            s, j = k // NJ, k % NJ
            g = STEPS[j]
            emit_scalar(k + S_AHEAD)
            emit_exp(k + S_AHEAD - 1)
            emit_mx(2 * k + 2)
            emit_mx(2 * k + 3)
            emit_evac(2 * k)
            if j > 0 and STEPS[j - 1] != BASE and on_vector(s, STEPS[j - 1]):
                emit_mult(s, STEPS[j - 1])
            if copy_due is not None:
                copy_due()
                copy_due = None
            if k in transposed:
                pe_part, v_part = transposed[k]
                copy_due = lambda v_part=v_part, ps=pe_part(): v_part(ps)
            for u in sums.get(k, []):
                emit_sum(*u)
            emit_evac(2 * k + 1)
            if k in quantise_at:
                quantise_at[k](0, SPAN)
            if k in outs:
                emit_out(outs[k])
            if g != BASE and not on_vector(s, g):
                emit_mult(s, g)
            if k in (2, 3):
                w_pair_quant(k)
        for k in range(NU, max(sums) + 1):
            for s, g in sums[k]:
                if g == G - 1:
                    emit_mult(s, g)
                emit_sum(s, g)
        emit_out(NSPAN - 1)
